import numpy as np
import ml_dtypes


def mxq(x, axis, fmt="e4m3"):
    dtype, down = {"e4m3": (ml_dtypes.float8_e4m3fn, 7), "e5m2": (ml_dtypes.float8_e5m2, 14)}[fmt]
    v = np.moveaxis(np.asarray(x, np.float32).astype(ml_dtypes.bfloat16).astype(np.float64), axis, -1)
    blocks = v.reshape(v.shape[:-1] + (-1, 32))
    amax = np.abs(blocks).max(-1, keepdims=True)
    byte = np.maximum(np.where(amax > 0, np.frexp(amax)[1] - 1 + 127, 0) - down, 1)
    scale = np.exp2(byte - 127.0)
    codes = (blocks / scale).astype(np.float32).astype(dtype).astype(np.float64)
    return np.moveaxis((codes * scale).reshape(v.shape), -1, axis)


WIDE = False


def mx_kscale(k):
    if not WIDE:
        return np.ones(k)
    levels = np.array([10, -10, 5, -5, 0])
    a = np.random.permutation(np.resize(levels, k // 512 * 4)).reshape(k // 512, 4)
    idx = np.arange(k)
    return np.exp2(a[idx // 512, idx % 128 // 32])


BF16 = ml_dtypes.bfloat16


def bf(x):
    return np.asarray(x, np.float32).astype(BF16)


def f64(x):
    return np.asarray(x).astype(np.float64)


B, NH, T, N = 1, 1, 1024, 512
THETA = 2.0 ** 16
STEP = 8


def rope(v, cos, sin):
    v_rot = np.stack((-v[..., 1::2], v[..., ::2]), axis=-1).reshape(v.shape)
    return v * cos + v_rot * sin


def setup_inputs():
    a, b = np.sqrt(11.0 / np.sqrt(N)), np.sqrt(1.4 / np.sqrt(N))
    q = a * np.random.standard_normal((B, NH, 1, N)) + b * np.random.standard_normal((B, NH, T, N))
    v = np.random.standard_normal((B, NH, T, N))
    omega = np.repeat(THETA ** (-np.arange(0, N, 2) / N), 2)
    phi = np.repeat(np.random.uniform(0.0, 2.0 * np.pi, N // 2), 2)
    ang = (np.arange(T)[:, None] * omega[None, :] + phi[None, :]).reshape(1, 1, T, N)
    s = mx_kscale(N)
    u = np.exp2(np.round(np.log2(s / s.max()) / 2))
    g = np.where((np.arange(T) % STEP == 0)[:, None], 1.0 / u[None, :], u[None, :]).reshape(1, 1, T, N)
    return {"Q": bf(q), "V": bf(v), "rope_cos": bf(np.cos(ang) * g), "rope_sin": bf(np.sin(ang) * g)}


def reference(Q, V, rope_cos, rope_sin):
    qr = rope(f64(Q), f64(rope_cos), f64(rope_sin))
    qrq = mxq(qr, 3, "e4m3")
    s = (qrq @ qrq.transpose(0, 1, 3, 2)) / np.sqrt(N)
    e = np.exp(s - s.max(-1, keepdims=True))
    return (mxq(e, 3, "e4m3") @ mxq(f64(V), 2, "e4m3")) / e.sum(-1, keepdims=True)

@@ -1,0 +1,257 @@
+import math
+
+import concourse.mybir as mybir
+from concourse.masks import make_identity
+
+F32 = mybir.dt.float32
+BF16 = mybir.dt.bfloat16
+U32 = mybir.dt.uint32
+U8 = mybir.dt.uint8
+FP8X4 = mybir.dt.float8_e4m3fn_x4
+ALU = mybir.AluOpType
+ACT = mybir.ActivationFunctionType
+
+P = 128
+T = 1024
+N = 512
+PACK = 4
+K_PASS = P * PACK
+BANK = 512
+CHUNKS = T // (2 * P)
+TILES = T // P
+KEY_PASSES = T // K_PASS
+FLOPS = 2 * 2 * T * T * N
+
+
+def first_column(m, j):
+    return K_PASS * (m // 2) + 2 * P * j + P * (m % 2)
+
+
+def tile_bidirectionalattentionv2_pa_kernel(tc, Q, V, rope_cos, rope_sin, out):
+    nc = tc.nc
+    by_chunk = "(m p j) f -> m p (j f)"
+    q_dram = Q.flatten_outer_dims().rearrange(by_chunk, m=CHUNKS, j=2)
+    cos_dram = rope_cos.flatten_outer_dims().rearrange(by_chunk, m=CHUNKS, j=2)
+    sin_dram = rope_sin.flatten_outer_dims().rearrange(by_chunk, m=CHUNKS, j=2)
+    v_dram = V.flatten_outer_dims().rearrange("(g p e u) f -> g u p e f", g=KEY_PASSES, e=2, u=2)
+    out_dram = out.flatten_outer_dims().rearrange("(m p j) f -> m j p f", m=CHUNKS, j=2)
+
+    with tc.tile_pool(name="keep", bufs=1) as keep, tc.tile_pool(name="rope", bufs=2) as rope_pool, tc.tile_pool(
+        name="soft", bufs=3
+    ) as soft, tc.tile_pool(name="stat", bufs=6) as stat, tc.psum_pool(name="score", bufs=4) as score_psum, tc.psum_pool(
+        name="flip", bufs=2
+    ) as flip_psum, tc.psum_pool(name="attend", bufs=2) as attend_psum:
+        q_sb, cos_sb, sin_sb, v_rows = {}, {}, {}, {}
+
+        def load_chunk(m):
+            q_sb[m] = keep.tile([P, 2 * N], BF16, name="q%d" % m)
+            cos_sb[m] = keep.tile([P, 2 * N], BF16, name="cos%d" % m)
+            sin_sb[m] = keep.tile([P, 2 * N], BF16, name="sin%d" % m)
+            nc.sync.dma_start(out=q_sb[m][:], in_=q_dram[m])
+            nc.sync.dma_start(out=cos_sb[m][:], in_=cos_dram[m])
+            nc.sync.dma_start(out=sin_sb[m][:], in_=sin_dram[m])
+
+        def load_v(g):
+            v_rows[g] = keep.tile([P, PACK, N], BF16, name="v_rows%d" % g)
+            for u in range(2):
+                nc.sync.dma_start(out=v_rows[g][:, 2 * u : 2 * u + 2, :], in_=v_dram[g][u])
+
+        for m in range(CHUNKS - 1):
+            load_chunk(m)
+        for g in range(KEY_PASSES):
+            load_v(g)
+        load_chunk(CHUNKS - 1)
+
+        ident = keep.tile([P, P], F32, name="ident")
+        make_identity(nc, ident[:])
+        zero = keep.tile([P, 1], F32, name="zero")
+        one = keep.tile([P, 1], F32, name="one")
+        nc.vector.memset(zero[:], 0.0)
+        nc.scalar.activation(out=one[:], in_=zero[:], func=ACT.Exp)
+
+        qr_pairs = keep.tile([P, T * 2], F32, name="qr_pairs", align_bytes=64)
+        qr_codes = keep.tile([P, T], U32, name="qr_codes", align_bytes=64)
+        qr_scales = keep.tile([P, T], U8, name="qr_scales", align_bytes=64)
+        v_codes = keep.tile([P, KEY_PASSES * N], U32, name="v_codes", align_bytes=64)
+        v_scales = keep.tile([P, KEY_PASSES * N], U8, name="v_scales", align_bytes=64)
+        v_grouped = {}
+
+        def rotate(m):
+            planes = "p (t i j) -> p t j i"
+            q = q_sb[m][:].rearrange(planes, t=2, j=2)
+            cos = cos_sb[m][:].rearrange(planes, t=2, j=2)
+            sin = sin_sb[m][:].rearrange(planes, t=2, j=2)
+            straight = rope_pool.tile([P, 2 * N], F32, name="straight")
+            crossed = rope_pool.tile([P, 2 * N], F32, name="crossed")
+            qr = rope_pool.tile([P, 2 * N], BF16, name="qr")
+            crossed_planes = crossed[:].rearrange("p (t j i) -> p t j i", t=2, j=2)
+            nc.vector.tensor_tensor(
+                out=straight[:].rearrange("p (t j i) -> p t j i", t=2, j=2), in0=q, in1=cos, op=ALU.mult
+            )
+            nc.vector.scalar_tensor_tensor(
+                out=crossed_planes[:, :, 0, :],
+                in0=q[:, :, 1, :],
+                scalar=-1.0,
+                in1=sin[:, :, 0, :],
+                op0=ALU.mult,
+                op1=ALU.mult,
+            )
+            nc.vector.tensor_tensor(out=crossed_planes[:, :, 1, :], in0=q[:, :, 0, :], in1=sin[:, :, 1, :], op=ALU.mult)
+            nc.vector.tensor_tensor(out=qr[:], in0=straight[:], in1=crossed[:], op=ALU.add)
+            return qr
+
+        def flip_qr(m, qr):
+            words = qr[:].bitcast(F32)
+            flipped = flip_psum.tile([P, BANK], F32, name="flipped")
+            for b in range(PACK):
+                nc.tensor.transpose(flipped[:, P * b : P * (b + 1)], words[:, P * b : P * (b + 1)], ident[:])
+            nc.scalar.copy(
+                out=qr_pairs[:].rearrange("p (g j h c u) -> p g h j c u", g=2, j=2, h=2, u=2)[:, m // 2, m % 2],
+                in_=flipped[:].rearrange("p (j u c) -> p j c u", j=2, u=2),
+            )
+
+        def quantise_qr(m):
+            for j in range(2):
+                c0 = first_column(m, j)
+                nc.vector.quantize_mx(
+                    out=qr_codes[:, c0 : c0 + P].bitcast(FP8X4),
+                    scales=qr_scales[:, c0 : c0 + P],
+                    in_=qr_pairs[:].bitcast(BF16)[:, PACK * c0 : PACK * (c0 + P)],
+                )
+
+        def regroup_v(g):
+            v_grouped[g] = keep.tile([P, N * PACK], BF16, name="v_grouped%d" % g, align_bytes=64)
+            nc.scalar.copy(
+                out=v_grouped[g][:].rearrange("p (c i t) -> p c t i", i=4, t=PACK),
+                in_=v_rows[g][:].rearrange("p t (c i) -> p c t i", i=4),
+            )
+
+        def quantise_v(g):
+            nc.vector.quantize_mx(
+                out=v_codes[:, N * g : N * (g + 1)].bitcast(FP8X4),
+                scales=v_scales[:, N * g : N * (g + 1)],
+                in_=v_grouped[g][:],
+            )
+
+        flip_qr(0, rotate(0))
+        flip_qr(1, rotate(1))
+        quantise_qr(0)
+        regroup_v(0)
+        flip_qr(2, rotate(2))
+        quantise_qr(1)
+        regroup_v(1)
+        flip_qr(3, rotate(3))
+        quantise_qr(2)
+        quantise_v(0)
+        quantise_v(1)
+        quantise_qr(3)
+
+        scores, shifted, lowest, e_sb, e_sum, e_flipped, e_codes, e_scales, attended = {}, {}, {}, {}, {}, {}, {}, {}, {}
+
+        def score(k):
+            scores[k] = []
+            for half in range(T // BANK):
+                bank = score_psum.tile([P, BANK], F32, name="bank")
+                nc.tensor.matmul_mx(
+                    out=bank[:],
+                    lhsT=qr_codes[:, P * k : P * (k + 1)].bitcast(FP8X4),
+                    lhsT_scale=qr_scales[:, P * k : P * (k + 1)],
+                    rhs=qr_codes[:, BANK * half : BANK * (half + 1)].bitcast(FP8X4),
+                    rhs_scale=qr_scales[:, BANK * half : BANK * (half + 1)],
+                    start=True,
+                    stop=True,
+                )
+                scores[k].append(bank)
+
+        def scale_and_min(k, half):
+            if half == 0:
+                shifted[k] = soft.tile([P, T], F32, name="shifted")
+                lowest[k] = stat.tile([P, T // BANK], F32, name="lowest")
+            nc.vector.tensor_scalar(
+                out=shifted[k][:, BANK * half : BANK * (half + 1)],
+                in0=scores[k][half][:],
+                scalar1=-1.0 / math.sqrt(N),
+                scalar2=None if half == 0 else lowest[k][:, half - 1 : half],
+                op0=ALU.mult,
+                op1=ALU.min,
+                accum_out=lowest[k][:, half : half + 1],
+            )
+
+        def exponential(k):
+            e_sb[k] = soft.tile([P, T], BF16, name="e_sb")
+            e_sum[k] = stat.tile([P, 1], F32, name="e_sum")
+            nc.scalar.activation(
+                out=e_sb[k][:],
+                in_=shifted[k][:],
+                func=ACT.Exp,
+                bias=lowest[k][:, T // BANK - 1 : T // BANK],
+                scale=-1.0,
+                accum_out=e_sum[k][:],
+            )
+
+        def flip_e(k):
+            words = e_sb[k][:].bitcast(F32)
+            e_flipped[k] = flip_psum.tile([P, BANK], F32, name="flipped")
+            for b in range(PACK):
+                nc.tensor.transpose(e_flipped[k][:, P * b : P * (b + 1)], words[:, P * b : P * (b + 1)], ident[:])
+
+        def pair_e(k):
+            e_pairs = soft.tile([P, BANK], F32, name="e_pairs", align_bytes=64)
+            nc.scalar.copy(
+                out=e_pairs[:].rearrange("p (g q u) -> p g q u", g=KEY_PASSES, u=2),
+                in_=e_flipped[k][:].rearrange("p (g u q) -> p g q u", g=KEY_PASSES, u=2),
+            )
+            return e_pairs
+
+        def quantise_e(k, e_pairs):
+            e_codes[k] = soft.tile([P, KEY_PASSES * P], U32, name="e_codes", align_bytes=64)
+            e_scales[k] = soft.tile([P, KEY_PASSES * P], U8, name="e_scales", align_bytes=64)
+            nc.vector.quantize_mx(
+                out=e_codes[k][:].bitcast(FP8X4), scales=e_scales[k][:], in_=e_pairs[:].bitcast(BF16)
+            )
+
+        def attend(k):
+            attended[k] = attend_psum.tile([P, N], F32, name="attended")
+            for g in range(KEY_PASSES):
+                nc.tensor.matmul_mx(
+                    out=attended[k][:],
+                    lhsT=e_codes[k][:, P * g : P * (g + 1)].bitcast(FP8X4),
+                    lhsT_scale=e_scales[k][:, P * g : P * (g + 1)],
+                    rhs=v_codes[:, N * g : N * (g + 1)].bitcast(FP8X4),
+                    rhs_scale=v_scales[:, N * g : N * (g + 1)],
+                    start=(g == 0),
+                    stop=(g == KEY_PASSES - 1),
+                )
+
+        def normalise_and_store(k):
+            inverse = stat.tile([P, 1], F32, name="inverse")
+            result = soft.tile([P, N], F32, name="result")
+            nc.vector.reciprocal(out=inverse[:], in_=e_sum[k][:])
+            if k % 2 == 0:
+                nc.vector.tensor_scalar(
+                    out=result[:], in0=attended[k][:], scalar1=inverse[:], scalar2=None, op0=ALU.mult
+                )
+            else:
+                nc.scalar.activation(out=result[:], in_=attended[k][:], func=ACT.Copy, scale=inverse[:])
+            m, j = 2 * (k // 4) + k % 2, (k // 2) % 2
+            nc.sync.dma_start(out=out_dram[m][j], in_=result[:])
+
+        score(0)
+        for s in range(TILES + 4):
+            if s + 1 < TILES:
+                score(s + 1)
+            if 0 <= s - 3 < TILES:
+                attend(s - 3)
+            if s < TILES:
+                scale_and_min(s, 0)
+            if 0 <= s - 1 < TILES:
+                exponential(s - 1)
+                flip_e(s - 1)
+            if 0 <= s - 2 < TILES:
+                e_pairs = pair_e(s - 2)
+            if 0 <= s - 3 < TILES:
+                normalise_and_store(s - 3)
+            if s < TILES:
+                scale_and_min(s, 1)
+            if 0 <= s - 2 < TILES:
+                quantise_e(s - 2, e_pairs)

@@ -51,16 +51,14 @@ def tile_bidirectionalattentionv2_pa_kernel(tc, Q, V, rope_cos, rope_sin, out):
             nc.sync.dma_start(out=cos_sb[m][:], in_=cos_dram[m])
             nc.sync.dma_start(out=sin_sb[m][:], in_=sin_dram[m])
 
-        def load_v(g):
-            v_rows[g] = keep.tile([P, PACK, N], BF16, name="v_rows%d" % g)
-            for u in range(2):
-                nc.sync.dma_start(out=v_rows[g][:, 2 * u : 2 * u + 2, :], in_=v_dram[g][u])
+        def load_v(g, u):
+            if u == 0:
+                v_rows[g] = keep.tile([P, PACK, N], BF16, name="v_rows%d" % g)
+            nc.sync.dma_start(out=v_rows[g][:, 2 * u : 2 * u + 2, :], in_=v_dram[g][u])
 
-        for m in range(CHUNKS - 1):
+        for m in range(CHUNKS):
             load_chunk(m)
-        for g in range(KEY_PASSES):
-            load_v(g)
-        load_chunk(CHUNKS - 1)
+            load_v(m // 2, m % 2)
 
         ident = keep.tile([P, P], F32, name="ident")
         make_identity(nc, ident[:])
@@ -69,7 +67,7 @@ def tile_bidirectionalattentionv2_pa_kernel(tc, Q, V, rope_cos, rope_sin, out):
         nc.vector.memset(zero[:], 0.0)
         nc.scalar.activation(out=one[:], in_=zero[:], func=ACT.Exp)
 
-        qr_pairs = keep.tile([P, T * 2], F32, name="qr_pairs", align_bytes=64)
+        qr_grouped = keep.tile([P, T * PACK], BF16, name="qr_grouped", align_bytes=64)
         qr_codes = keep.tile([P, T], U32, name="qr_codes", align_bytes=64)
         qr_scales = keep.tile([P, T], U8, name="qr_scales", align_bytes=64)
         v_codes = keep.tile([P, KEY_PASSES * N], U32, name="v_codes", align_bytes=64)
@@ -77,46 +75,56 @@ def tile_bidirectionalattentionv2_pa_kernel(tc, Q, V, rope_cos, rope_sin, out):
         v_grouped = {}
 
         def rotate(m):
-            planes = "p (t i j) -> p t j i"
-            q = q_sb[m][:].rearrange(planes, t=2, j=2)
-            cos = cos_sb[m][:].rearrange(planes, t=2, j=2)
-            sin = sin_sb[m][:].rearrange(planes, t=2, j=2)
+            split = "p (x h j) -> p j h x"
+            q = q_sb[m][:].rearrange(split, h=2, j=2)
+            cos = cos_sb[m][:].rearrange(split, h=2, j=2)
+            sin = sin_sb[m][:].rearrange(split, h=2, j=2)
             straight = rope_pool.tile([P, 2 * N], F32, name="straight")
             crossed = rope_pool.tile([P, 2 * N], F32, name="crossed")
-            qr = rope_pool.tile([P, 2 * N], BF16, name="qr")
-            crossed_planes = crossed[:].rearrange("p (t j i) -> p t j i", t=2, j=2)
             nc.vector.tensor_tensor(
-                out=straight[:].rearrange("p (t j i) -> p t j i", t=2, j=2), in0=q, in1=cos, op=ALU.mult
+                out=straight[:].rearrange("p (j h x) -> p j h x", j=2, h=2), in0=q, in1=cos, op=ALU.mult
             )
+            crossed_halves = crossed[:].rearrange("p (j h x) -> p j h x", j=2, h=2)
             nc.vector.scalar_tensor_tensor(
-                out=crossed_planes[:, :, 0, :],
-                in0=q[:, :, 1, :],
-                scalar=-1.0,
-                in1=sin[:, :, 0, :],
-                op0=ALU.mult,
-                op1=ALU.mult,
+                out=crossed_halves[:, 0], in0=q[:, 1], scalar=-1.0, in1=sin[:, 0], op0=ALU.mult, op1=ALU.mult
             )
-            nc.vector.tensor_tensor(out=crossed_planes[:, :, 1, :], in0=q[:, :, 0, :], in1=sin[:, :, 1, :], op=ALU.mult)
-            nc.vector.tensor_tensor(out=qr[:], in0=straight[:], in1=crossed[:], op=ALU.add)
-            return qr
+            nc.vector.tensor_tensor(out=crossed_halves[:, 1], in0=q[:, 0], in1=sin[:, 1], op=ALU.mult)
+            return straight, crossed
 
-        def flip_qr(m, qr):
-            words = qr[:].bitcast(F32)
-            flipped = flip_psum.tile([P, BANK], F32, name="flipped")
-            for b in range(PACK):
-                nc.tensor.transpose(flipped[:, P * b : P * (b + 1)], words[:, P * b : P * (b + 1)], ident[:])
-            nc.scalar.copy(
-                out=qr_pairs[:].rearrange("p (g j h c u) -> p g h j c u", g=2, j=2, h=2, u=2)[:, m // 2, m % 2],
-                in_=flipped[:].rearrange("p (j u c) -> p j c u", j=2, u=2),
-            )
+        def add_and_flip_qr(m, straight, crossed):
+            for i in range(2):
+                summed = score_psum.tile([P, BANK], F32, name="bank")
+                for t in range(PACK):
+                    first = 2 * P * (2 * (t % 2) + t // 2) + P * i
+                    nc.tensor.matmul(
+                        out=summed[:, P * t : P * (t + 1)],
+                        lhsT=straight[:, first : first + P],
+                        rhs=ident[:],
+                        start=True,
+                        stop=False,
+                        is_transpose=True,
+                    )
+                    nc.tensor.matmul(
+                        out=summed[:, P * t : P * (t + 1)],
+                        lhsT=crossed[:, first : first + P],
+                        rhs=ident[:],
+                        start=False,
+                        stop=True,
+                        is_transpose=True,
+                    )
+                c0 = first_column(m, i)
+                nc.scalar.copy(
+                    out=qr_grouped[:, PACK * c0 : PACK * (c0 + P)].rearrange("p (c t) -> p c t", t=PACK),
+                    in_=summed[:].rearrange("p (t c) -> p c t", t=PACK),
+                )
 
         def quantise_qr(m):
-            for j in range(2):
-                c0 = first_column(m, j)
+            for i in range(2):
+                c0 = first_column(m, i)
                 nc.vector.quantize_mx(
                     out=qr_codes[:, c0 : c0 + P].bitcast(FP8X4),
                     scales=qr_scales[:, c0 : c0 + P],
-                    in_=qr_pairs[:].bitcast(BF16)[:, PACK * c0 : PACK * (c0 + P)],
+                    in_=qr_grouped[:, PACK * c0 : PACK * (c0 + P)],
                 )
 
         def regroup_v(g):
@@ -133,18 +141,16 @@ def tile_bidirectionalattentionv2_pa_kernel(tc, Q, V, rope_cos, rope_sin, out):
                 in_=v_grouped[g][:],
             )
 
-        flip_qr(0, rotate(0))
-        flip_qr(1, rotate(1))
-        quantise_qr(0)
-        regroup_v(0)
-        flip_qr(2, rotate(2))
-        quantise_qr(1)
-        regroup_v(1)
-        flip_qr(3, rotate(3))
-        quantise_qr(2)
+        for m in range(CHUNKS):
+            straight, crossed = rotate(m)
+            add_and_flip_qr(m, straight, crossed)
+            if m == 0:
+                regroup_v(0)
+            else:
+                quantise_qr(m - 1)
         quantise_v(0)
-        quantise_v(1)
-        quantise_qr(3)
+        quantise_qr(CHUNKS - 1)
+        regroup_v(1)
 
         scores, shifted, lowest, e_sb, e_sum, e_flipped, e_codes, e_scales, attended = {}, {}, {}, {}, {}, {}, {}, {}, {}
 
@@ -236,22 +242,24 @@ def tile_bidirectionalattentionv2_pa_kernel(tc, Q, V, rope_cos, rope_sin, out):
             m, j = 2 * (k // 4) + k % 2, (k // 2) % 2
             nc.sync.dma_start(out=out_dram[m][j], in_=result[:])
 
+        e_pairs = {}
         score(0)
-        for s in range(TILES + 4):
+        for s in range(TILES + 5):
             if s + 1 < TILES:
                 score(s + 1)
-            if 0 <= s - 3 < TILES:
-                attend(s - 3)
             if s < TILES:
                 scale_and_min(s, 0)
+            if s - 3 == 0:
+                quantise_v(1)
+            if 0 <= s - 3 < TILES:
+                quantise_e(s - 3, e_pairs[s - 3])
+                attend(s - 3)
+            if s < TILES:
+                scale_and_min(s, 1)
             if 0 <= s - 1 < TILES:
                 exponential(s - 1)
                 flip_e(s - 1)
             if 0 <= s - 2 < TILES:
-                e_pairs = pair_e(s - 2)
-            if 0 <= s - 3 < TILES:
-                normalise_and_store(s - 3)
-            if s < TILES:
-                scale_and_min(s, 1)
-            if 0 <= s - 2 < TILES:
-                quantise_e(s - 2, e_pairs)
+                e_pairs[s - 2] = pair_e(s - 2)
+            if 0 <= s - 4 < TILES:
+                normalise_and_store(s - 4)

@@ -19,46 +19,48 @@ K_PASS = P * PACK
 BANK = 512
 CHUNKS = T // (2 * P)
 TILES = T // P
+HALVES = T // BANK
 KEY_PASSES = T // K_PASS
 FLOPS = 2 * 2 * T * T * N
 
+QR_LAG = 3
+EXP_LAG = 1
+PAIR_LAG = 2
+QUANTISE_LAG = 3
+OUTPUT_LAG = 4
 
-def first_column(m, j):
-    return K_PASS * (m // 2) + 2 * P * j + P * (m % 2)
+
+def first_column(n):
+    m, i = n // 2, n % 2
+    return K_PASS * (m // 2) + 2 * P * i + P * (m % 2)
 
 
 def tile_bidirectionalattentionv2_pa_kernel(tc, Q, V, rope_cos, rope_sin, out):
     nc = tc.nc
-    by_chunk = "(m p j) f -> m p (j f)"
-    q_dram = Q.flatten_outer_dims().rearrange(by_chunk, m=CHUNKS, j=2)
-    cos_dram = rope_cos.flatten_outer_dims().rearrange(by_chunk, m=CHUNKS, j=2)
-    sin_dram = rope_sin.flatten_outer_dims().rearrange(by_chunk, m=CHUNKS, j=2)
+    by_chunk = "(m p i) f -> m p (i f)"
+    q_dram = Q.flatten_outer_dims().rearrange(by_chunk, m=CHUNKS, i=2)
+    cos_dram = rope_cos.flatten_outer_dims().rearrange(by_chunk, m=CHUNKS, i=2)
+    sin_dram = rope_sin.flatten_outer_dims().rearrange(by_chunk, m=CHUNKS, i=2)
     v_dram = V.flatten_outer_dims().rearrange("(g p e u) f -> g u p e f", g=KEY_PASSES, e=2, u=2)
-    out_dram = out.flatten_outer_dims().rearrange("(m p j) f -> m j p f", m=CHUNKS, j=2)
+    out_dram = out.flatten_outer_dims().rearrange("(m p i) f -> m i p f", m=CHUNKS, i=2)
 
-    with tc.tile_pool(name="keep", bufs=1) as keep, tc.tile_pool(name="rope", bufs=2) as rope_pool, tc.tile_pool(
-        name="soft", bufs=3
-    ) as soft, tc.tile_pool(name="stat", bufs=6) as stat, tc.psum_pool(name="score", bufs=4) as score_psum, tc.psum_pool(
+    with tc.tile_pool(name="keep", bufs=1) as keep, tc.tile_pool(name="rope", bufs=4) as rope_pool, tc.tile_pool(
+        name="soft", bufs=4
+    ) as soft, tc.tile_pool(name="stat", bufs=TILES) as stat, tc.psum_pool(name="score", bufs=4) as score_psum, tc.psum_pool(
         name="flip", bufs=2
-    ) as flip_psum, tc.psum_pool(name="attend", bufs=2) as attend_psum:
+    ) as flip_psum, tc.psum_pool(name="attend", bufs=2) as attend_psum, tc.manual_schedule():
         q_sb, cos_sb, sin_sb, v_rows = {}, {}, {}, {}
-
-        def load_chunk(m):
+        for m in range(CHUNKS):
             q_sb[m] = keep.tile([P, 2 * N], BF16, name="q%d" % m)
             cos_sb[m] = keep.tile([P, 2 * N], BF16, name="cos%d" % m)
             sin_sb[m] = keep.tile([P, 2 * N], BF16, name="sin%d" % m)
             nc.sync.dma_start(out=q_sb[m][:], in_=q_dram[m])
             nc.sync.dma_start(out=cos_sb[m][:], in_=cos_dram[m])
             nc.sync.dma_start(out=sin_sb[m][:], in_=sin_dram[m])
-
-        def load_v(g, u):
-            if u == 0:
-                v_rows[g] = keep.tile([P, PACK, N], BF16, name="v_rows%d" % g)
-            nc.sync.dma_start(out=v_rows[g][:, 2 * u : 2 * u + 2, :], in_=v_dram[g][u])
-
-        for m in range(CHUNKS):
-            load_chunk(m)
-            load_v(m // 2, m % 2)
+        for g in range(KEY_PASSES):
+            v_rows[g] = keep.tile([P, PACK, N], BF16, name="v_rows%d" % g)
+            for u in range(2):
+                nc.sync.dma_start(out=v_rows[g][:, 2 * u : 2 * u + 2, :], in_=v_dram[g][u])
 
         ident = keep.tile([P, P], F32, name="ident")
         make_identity(nc, ident[:])
@@ -70,32 +72,28 @@ def tile_bidirectionalattentionv2_pa_kernel(tc, Q, V, rope_cos, rope_sin, out):
         qr_grouped = keep.tile([P, T * PACK], BF16, name="qr_grouped", align_bytes=64)
         qr_codes = keep.tile([P, T], U32, name="qr_codes", align_bytes=64)
         qr_scales = keep.tile([P, T], U8, name="qr_scales", align_bytes=64)
-        v_codes = keep.tile([P, KEY_PASSES * N], U32, name="v_codes", align_bytes=64)
-        v_scales = keep.tile([P, KEY_PASSES * N], U8, name="v_scales", align_bytes=64)
-        v_grouped = {}
 
-        def rotate(m):
-            split = "p (x h j) -> p j h x"
-            q = q_sb[m][:].rearrange(split, h=2, j=2)
-            cos = cos_sb[m][:].rearrange(split, h=2, j=2)
-            sin = sin_sb[m][:].rearrange(split, h=2, j=2)
-            straight = rope_pool.tile([P, 2 * N], F32, name="straight")
-            crossed = rope_pool.tile([P, 2 * N], F32, name="crossed")
+        def rotate(n):
+            m, i = n // 2, n % 2
+            split = "p (a h j) -> p j h a"
+            q = q_sb[m][:, N * i : N * (i + 1)].rearrange(split, h=2, j=2)
+            cos = cos_sb[m][:, N * i : N * (i + 1)].rearrange(split, h=2, j=2)
+            sin = sin_sb[m][:, N * i : N * (i + 1)].rearrange(split, h=2, j=2)
+            straight = rope_pool.tile([P, N], F32, name="straight")
+            crossed = rope_pool.tile([P, N], F32, name="crossed")
+            crossed_halves = crossed[:].rearrange("p (j h a) -> p j h a", j=2, h=2)
             nc.vector.tensor_tensor(
-                out=straight[:].rearrange("p (j h x) -> p j h x", j=2, h=2), in0=q, in1=cos, op=ALU.mult
+                out=straight[:].rearrange("p (j h a) -> p j h a", j=2, h=2), in0=q, in1=cos, op=ALU.mult
             )
-            crossed_halves = crossed[:].rearrange("p (j h x) -> p j h x", j=2, h=2)
             nc.vector.scalar_tensor_tensor(
                 out=crossed_halves[:, 0], in0=q[:, 1], scalar=-1.0, in1=sin[:, 0], op0=ALU.mult, op1=ALU.mult
             )
             nc.vector.tensor_tensor(out=crossed_halves[:, 1], in0=q[:, 0], in1=sin[:, 1], op=ALU.mult)
-            return straight, crossed
-
-        def add_and_flip_qr(m, straight, crossed):
-            for i in range(2):
-                summed = score_psum.tile([P, BANK], F32, name="bank")
-                for t in range(PACK):
-                    first = 2 * P * (2 * (t % 2) + t // 2) + P * i
+            summed = flip_psum.tile([P, BANK], F32, name="flipped")
+            for j in range(2):
+                for h in range(2):
+                    t = 2 * h + j
+                    first = P * (2 * j + h)
                     nc.tensor.matmul(
                         out=summed[:, P * t : P * (t + 1)],
                         lhsT=straight[:, first : first + P],
@@ -112,24 +110,27 @@ def tile_bidirectionalattentionv2_pa_kernel(tc, Q, V, rope_cos, rope_sin, out):
                         stop=True,
                         is_transpose=True,
                     )
-                c0 = first_column(m, i)
-                nc.scalar.copy(
-                    out=qr_grouped[:, PACK * c0 : PACK * (c0 + P)].rearrange("p (c t) -> p c t", t=PACK),
-                    in_=summed[:].rearrange("p (t c) -> p c t", t=PACK),
-                )
-
-        def quantise_qr(m):
-            for i in range(2):
-                c0 = first_column(m, i)
-                nc.vector.quantize_mx(
-                    out=qr_codes[:, c0 : c0 + P].bitcast(FP8X4),
-                    scales=qr_scales[:, c0 : c0 + P],
-                    in_=qr_grouped[:, PACK * c0 : PACK * (c0 + P)],
-                )
-
-        def regroup_v(g):
-            v_grouped[g] = keep.tile([P, N * PACK], BF16, name="v_grouped%d" % g, align_bytes=64)
+            c0 = first_column(n)
             nc.scalar.copy(
+                out=qr_grouped[:, PACK * c0 : PACK * (c0 + P)].rearrange("p (c t) -> p c t", t=PACK),
+                in_=summed[:].rearrange("p (t c) -> p c t", t=PACK),
+            )
+
+        def quantise_qr(n):
+            c0 = first_column(n)
+            nc.vector.quantize_mx(
+                out=qr_codes[:, c0 : c0 + P].bitcast(FP8X4),
+                scales=qr_scales[:, c0 : c0 + P],
+                in_=qr_grouped[:, PACK * c0 : PACK * (c0 + P)],
+            )
+
+        v_codes = keep.tile([P, KEY_PASSES * N], U32, name="v_codes", align_bytes=64)
+        v_scales = keep.tile([P, KEY_PASSES * N], U8, name="v_scales", align_bytes=64)
+        v_grouped = {}
+
+        def regroup_v(g, copy):
+            v_grouped[g] = keep.tile([P, N * PACK], BF16, name="v_grouped%d" % g, align_bytes=64)
+            copy(
                 out=v_grouped[g][:].rearrange("p (c i t) -> p c t i", i=4, t=PACK),
                 in_=v_rows[g][:].rearrange("p t (c i) -> p c t i", i=4),
             )
@@ -141,41 +142,29 @@ def tile_bidirectionalattentionv2_pa_kernel(tc, Q, V, rope_cos, rope_sin, out):
                 in_=v_grouped[g][:],
             )
 
-        for m in range(CHUNKS):
-            straight, crossed = rotate(m)
-            add_and_flip_qr(m, straight, crossed)
-            if m == 0:
-                regroup_v(0)
-            else:
-                quantise_qr(m - 1)
-        quantise_v(0)
-        quantise_qr(CHUNKS - 1)
-        regroup_v(1)
+        banks, shifted, lowest, e_sb, e_sum, e_flipped, e_pairs, e_codes, e_scales, attended = (
+            {}, {}, {}, {}, {}, {}, {}, {}, {}, {},
+        )
 
-        scores, shifted, lowest, e_sb, e_sum, e_flipped, e_codes, e_scales, attended = {}, {}, {}, {}, {}, {}, {}, {}, {}
-
-        def score(k):
-            scores[k] = []
-            for half in range(T // BANK):
-                bank = score_psum.tile([P, BANK], F32, name="bank")
-                nc.tensor.matmul_mx(
-                    out=bank[:],
-                    lhsT=qr_codes[:, P * k : P * (k + 1)].bitcast(FP8X4),
-                    lhsT_scale=qr_scales[:, P * k : P * (k + 1)],
-                    rhs=qr_codes[:, BANK * half : BANK * (half + 1)].bitcast(FP8X4),
-                    rhs_scale=qr_scales[:, BANK * half : BANK * (half + 1)],
-                    start=True,
-                    stop=True,
-                )
-                scores[k].append(bank)
+        def score(k, half):
+            banks[k, half] = score_psum.tile([P, BANK], F32, name="bank")
+            nc.tensor.matmul_mx(
+                out=banks[k, half][:],
+                lhsT=qr_codes[:, P * k : P * (k + 1)].bitcast(FP8X4),
+                lhsT_scale=qr_scales[:, P * k : P * (k + 1)],
+                rhs=qr_codes[:, BANK * half : BANK * (half + 1)].bitcast(FP8X4),
+                rhs_scale=qr_scales[:, BANK * half : BANK * (half + 1)],
+                start=True,
+                stop=True,
+            )
 
         def scale_and_min(k, half):
             if half == 0:
                 shifted[k] = soft.tile([P, T], F32, name="shifted")
-                lowest[k] = stat.tile([P, T // BANK], F32, name="lowest")
+                lowest[k] = stat.tile([P, HALVES], F32, name="lowest")
             nc.vector.tensor_scalar(
                 out=shifted[k][:, BANK * half : BANK * (half + 1)],
-                in0=scores[k][half][:],
+                in0=banks[k, half][:],
                 scalar1=-1.0 / math.sqrt(N),
                 scalar2=None if half == 0 else lowest[k][:, half - 1 : half],
                 op0=ALU.mult,
@@ -190,7 +179,7 @@ def tile_bidirectionalattentionv2_pa_kernel(tc, Q, V, rope_cos, rope_sin, out):
                 out=e_sb[k][:],
                 in_=shifted[k][:],
                 func=ACT.Exp,
-                bias=lowest[k][:, T // BANK - 1 : T // BANK],
+                bias=lowest[k][:, HALVES - 1 : HALVES],
                 scale=-1.0,
                 accum_out=e_sum[k][:],
             )
@@ -202,18 +191,17 @@ def tile_bidirectionalattentionv2_pa_kernel(tc, Q, V, rope_cos, rope_sin, out):
                 nc.tensor.transpose(e_flipped[k][:, P * b : P * (b + 1)], words[:, P * b : P * (b + 1)], ident[:])
 
         def pair_e(k):
-            e_pairs = soft.tile([P, BANK], F32, name="e_pairs", align_bytes=64)
+            e_pairs[k] = soft.tile([P, BANK], F32, name="e_pairs", align_bytes=64)
             nc.scalar.copy(
-                out=e_pairs[:].rearrange("p (g q u) -> p g q u", g=KEY_PASSES, u=2),
+                out=e_pairs[k][:].rearrange("p (g q u) -> p g q u", g=KEY_PASSES, u=2),
                 in_=e_flipped[k][:].rearrange("p (g u q) -> p g q u", g=KEY_PASSES, u=2),
             )
-            return e_pairs
 
-        def quantise_e(k, e_pairs):
+        def quantise_e(k):
             e_codes[k] = soft.tile([P, KEY_PASSES * P], U32, name="e_codes", align_bytes=64)
             e_scales[k] = soft.tile([P, KEY_PASSES * P], U8, name="e_scales", align_bytes=64)
             nc.vector.quantize_mx(
-                out=e_codes[k][:].bitcast(FP8X4), scales=e_scales[k][:], in_=e_pairs[:].bitcast(BF16)
+                out=e_codes[k][:].bitcast(FP8X4), scales=e_scales[k][:], in_=e_pairs[k][:].bitcast(BF16)
             )
 
         def attend(k):
@@ -233,33 +221,41 @@ def tile_bidirectionalattentionv2_pa_kernel(tc, Q, V, rope_cos, rope_sin, out):
             inverse = stat.tile([P, 1], F32, name="inverse")
             result = soft.tile([P, N], F32, name="result")
             nc.vector.reciprocal(out=inverse[:], in_=e_sum[k][:])
-            if k % 2 == 0:
-                nc.vector.tensor_scalar(
-                    out=result[:], in0=attended[k][:], scalar1=inverse[:], scalar2=None, op0=ALU.mult
-                )
-            else:
-                nc.scalar.activation(out=result[:], in_=attended[k][:], func=ACT.Copy, scale=inverse[:])
-            m, j = 2 * (k // 4) + k % 2, (k // 2) % 2
-            nc.sync.dma_start(out=out_dram[m][j], in_=result[:])
+            nc.vector.tensor_scalar(out=result[:], in0=attended[k][:], scalar1=inverse[:], scalar2=None, op0=ALU.mult)
+            m, i = 2 * (k // 4) + k % 2, (k // 2) % 2
+            nc.sync.dma_start(out=out_dram[m][i], in_=result[:])
 
-        e_pairs = {}
-        score(0)
-        for s in range(TILES + 5):
+        for n in range(TILES):
+            rotate(n)
+            if n >= QR_LAG:
+                quantise_qr(n - QR_LAG)
+        quantise_qr(TILES - 3)
+        regroup_v(0, nc.vector.tensor_copy)
+        quantise_v(0)
+        quantise_qr(TILES - 2)
+        score(0, 0)
+        score(1, 0)
+        scale_and_min(0, 0)
+        quantise_qr(TILES - 1)
+        regroup_v(1, nc.scalar.copy)
+        score(0, 1)
+        for s in range(TILES + OUTPUT_LAG):
+            if s + 2 < TILES:
+                score(s + 2, 0)
             if s + 1 < TILES:
-                score(s + 1)
-            if s < TILES:
-                scale_and_min(s, 0)
-            if s - 3 == 0:
+                score(s + 1, 1)
+                scale_and_min(s + 1, 0)
+            if s == QUANTISE_LAG - 1:
                 quantise_v(1)
-            if 0 <= s - 3 < TILES:
-                quantise_e(s - 3, e_pairs[s - 3])
-                attend(s - 3)
+            if 0 <= s - QUANTISE_LAG < TILES:
+                quantise_e(s - QUANTISE_LAG)
+                attend(s - QUANTISE_LAG)
             if s < TILES:
                 scale_and_min(s, 1)
-            if 0 <= s - 1 < TILES:
-                exponential(s - 1)
-                flip_e(s - 1)
-            if 0 <= s - 2 < TILES:
-                e_pairs[s - 2] = pair_e(s - 2)
-            if 0 <= s - 4 < TILES:
-                normalise_and_store(s - 4)
+            if 0 <= s - EXP_LAG < TILES:
+                exponential(s - EXP_LAG)
+                flip_e(s - EXP_LAG)
+            if 0 <= s - PAIR_LAG < TILES:
+                pair_e(s - PAIR_LAG)
+            if 0 <= s - OUTPUT_LAG < TILES:
+                normalise_and_store(s - OUTPUT_LAG)

@@ -23,7 +23,7 @@ HALVES = T // BANK
 KEY_PASSES = T // K_PASS
 FLOPS = 2 * 2 * T * T * N
 
-QR_LAG = 3
+COPY_AHEAD = 2
 EXP_LAG = 1
 PAIR_LAG = 2
 QUANTISE_LAG = 3
@@ -64,6 +64,8 @@ def tile_bidirectionalattentionv2_pa_kernel(tc, Q, V, rope_cos, rope_sin, out):
 
         ident = keep.tile([P, P], F32, name="ident")
         make_identity(nc, ident[:])
+        ident_bf = keep.tile([P, P], BF16, name="ident_bf")
+        make_identity(nc, ident_bf[:])
         zero = keep.tile([P, 1], F32, name="zero")
         one = keep.tile([P, 1], F32, name="one")
         nc.vector.memset(zero[:], 0.0)
@@ -73,10 +75,20 @@ def tile_bidirectionalattentionv2_pa_kernel(tc, Q, V, rope_cos, rope_sin, out):
         qr_codes = keep.tile([P, T], U32, name="qr_codes", align_bytes=64)
         qr_scales = keep.tile([P, T], U8, name="qr_scales", align_bytes=64)
 
+        q_psum = {}
+
+        def copy_q(n):
+            m, i = n // 2, n % 2
+            q_psum[n] = score_psum.tile([P, BANK], F32, name="bank")
+            nc.tensor.matmul(
+                out=q_psum[n][:], lhsT=ident_bf[:], rhs=q_sb[m][:, N * i : N * (i + 1)], start=True, stop=True
+            )
+
         def rotate(n):
             m, i = n // 2, n % 2
             split = "p (a h j) -> p j h a"
-            q = q_sb[m][:, N * i : N * (i + 1)].rearrange(split, h=2, j=2)
+            q = q_psum[n][:].rearrange(split, h=2, j=2)
+            q_in_sbuf = q_sb[m][:, N * i : N * (i + 1)].rearrange(split, h=2, j=2)
             cos = cos_sb[m][:, N * i : N * (i + 1)].rearrange(split, h=2, j=2)
             sin = sin_sb[m][:, N * i : N * (i + 1)].rearrange(split, h=2, j=2)
             straight = rope_pool.tile([P, N], F32, name="straight")
@@ -88,7 +100,7 @@ def tile_bidirectionalattentionv2_pa_kernel(tc, Q, V, rope_cos, rope_sin, out):
             nc.vector.scalar_tensor_tensor(
                 out=crossed_halves[:, 0], in0=q[:, 1], scalar=-1.0, in1=sin[:, 0], op0=ALU.mult, op1=ALU.mult
             )
-            nc.vector.tensor_tensor(out=crossed_halves[:, 1], in0=q[:, 0], in1=sin[:, 1], op=ALU.mult)
+            nc.gpsimd.tensor_tensor(out=crossed_halves[:, 1], in0=q_in_sbuf[:, 0], in1=sin[:, 1], op=ALU.mult)
             summed = flip_psum.tile([P, BANK], F32, name="flipped")
             for j in range(2):
                 for h in range(2):
@@ -225,16 +237,18 @@ def tile_bidirectionalattentionv2_pa_kernel(tc, Q, V, rope_cos, rope_sin, out):
             m, i = 2 * (k // 4) + k % 2, (k // 2) % 2
             nc.sync.dma_start(out=out_dram[m][i], in_=result[:])
 
+        for n in range(COPY_AHEAD):
+            copy_q(n)
         for n in range(TILES):
+            if n + COPY_AHEAD < TILES:
+                copy_q(n + COPY_AHEAD)
             rotate(n)
-            if n >= QR_LAG:
-                quantise_qr(n - QR_LAG)
-        quantise_qr(TILES - 3)
-        regroup_v(0, nc.vector.tensor_copy)
-        quantise_v(0)
-        quantise_qr(TILES - 2)
+        for n in range(TILES - 2):
+            quantise_qr(n)
         score(0, 0)
         score(1, 0)
+        regroup_v(0, nc.vector.tensor_copy)
+        quantise_qr(TILES - 2)
         scale_and_min(0, 0)
         quantise_qr(TILES - 1)
         regroup_v(1, nc.scalar.copy)
@@ -245,8 +259,8 @@ def tile_bidirectionalattentionv2_pa_kernel(tc, Q, V, rope_cos, rope_sin, out):
             if s + 1 < TILES:
                 score(s + 1, 1)
                 scale_and_min(s + 1, 0)
-            if s == QUANTISE_LAG - 1:
-                quantise_v(1)
+            if s % 2 == 0 and s < QUANTISE_LAG:
+                quantise_v(s // 2)
             if 0 <= s - QUANTISE_LAG < TILES:
                 quantise_e(s - QUANTISE_LAG)
                 attend(s - QUANTISE_LAG)

@@ -26,8 +26,8 @@ FLOPS = 2 * 2 * T * T * N
 COPY_AHEAD = 2
 EXP_LAG = 1
 PAIR_LAG = 2
-QUANTISE_LAG = 3
-OUTPUT_LAG = 4
+QUANTISE_LAG = 4
+OUTPUT_LAG = 5
 
 
 def first_column(n):
@@ -47,8 +47,8 @@ def tile_bidirectionalattentionv2_pa_kernel(tc, Q, V, rope_cos, rope_sin, out):
     with tc.tile_pool(name="keep", bufs=1) as keep, tc.tile_pool(name="rope", bufs=4) as rope_pool, tc.tile_pool(
         name="soft", bufs=4
     ) as soft, tc.tile_pool(name="stat", bufs=TILES) as stat, tc.psum_pool(name="score", bufs=4) as score_psum, tc.psum_pool(
-        name="flip", bufs=2
-    ) as flip_psum, tc.psum_pool(name="attend", bufs=2) as attend_psum, tc.manual_schedule():
+        name="other", bufs=4
+    ) as other_psum, tc.manual_schedule():
         q_sb, cos_sb, sin_sb, v_rows = {}, {}, {}, {}
         for m in range(CHUNKS):
             q_sb[m] = keep.tile([P, 2 * N], BF16, name="q%d" % m)
@@ -101,7 +101,7 @@ def tile_bidirectionalattentionv2_pa_kernel(tc, Q, V, rope_cos, rope_sin, out):
                 out=crossed_halves[:, 0], in0=q[:, 1], scalar=-1.0, in1=sin[:, 0], op0=ALU.mult, op1=ALU.mult
             )
             nc.gpsimd.tensor_tensor(out=crossed_halves[:, 1], in0=q_in_sbuf[:, 0], in1=sin[:, 1], op=ALU.mult)
-            summed = flip_psum.tile([P, BANK], F32, name="flipped")
+            summed = other_psum.tile([P, BANK], F32, name="other")
             for j in range(2):
                 for h in range(2):
                     t = 2 * h + j
@@ -198,7 +198,7 @@ def tile_bidirectionalattentionv2_pa_kernel(tc, Q, V, rope_cos, rope_sin, out):
 
         def flip_e(k):
             words = e_sb[k][:].bitcast(F32)
-            e_flipped[k] = flip_psum.tile([P, BANK], F32, name="flipped")
+            e_flipped[k] = other_psum.tile([P, BANK], F32, name="other")
             for b in range(PACK):
                 nc.tensor.transpose(e_flipped[k][:, P * b : P * (b + 1)], words[:, P * b : P * (b + 1)], ident[:])
 
@@ -217,7 +217,7 @@ def tile_bidirectionalattentionv2_pa_kernel(tc, Q, V, rope_cos, rope_sin, out):
             )
 
         def attend(k):
-            attended[k] = attend_psum.tile([P, N], F32, name="attended")
+            attended[k] = other_psum.tile([P, N], F32, name="other")
             for g in range(KEY_PASSES):
                 nc.tensor.matmul_mx(
                     out=attended[k][:],

@@ -24,10 +24,10 @@ KEY_PASSES = T // K_PASS
 FLOPS = 2 * 2 * T * T * N
 
 COPY_AHEAD = 2
-EXP_LAG = 1
-PAIR_LAG = 2
-QUANTISE_LAG = 4
-OUTPUT_LAG = 5
+ATTEND_LAG = 3
+QUANTISE_LAG = 3
+OUTPUT_LAG = 4
+EARLY = 4
 
 
 def first_column(n):
@@ -50,17 +50,24 @@ def tile_bidirectionalattentionv2_pa_kernel(tc, Q, V, rope_cos, rope_sin, out):
         name="other", bufs=4
     ) as other_psum, tc.manual_schedule():
         q_sb, cos_sb, sin_sb, v_rows = {}, {}, {}, {}
+
+        def load_v(g):
+            v_rows[g] = keep.tile([P, PACK, N], BF16, name="v_rows%d" % g)
+            for u in range(2):
+                nc.sync.dma_start(out=v_rows[g][:, 2 * u : 2 * u + 2, :], in_=v_dram[g][u])
+
         for m in range(CHUNKS):
             q_sb[m] = keep.tile([P, 2 * N], BF16, name="q%d" % m)
             cos_sb[m] = keep.tile([P, 2 * N], BF16, name="cos%d" % m)
             sin_sb[m] = keep.tile([P, 2 * N], BF16, name="sin%d" % m)
-            nc.sync.dma_start(out=q_sb[m][:], in_=q_dram[m])
-            nc.sync.dma_start(out=cos_sb[m][:], in_=cos_dram[m])
-            nc.sync.dma_start(out=sin_sb[m][:], in_=sin_dram[m])
+            width = N if m < 4 else 2 * N
+            for first in range(0, 2 * N, width):
+                cols = slice(first, first + width)
+                nc.sync.dma_start(out=q_sb[m][:, cols], in_=q_dram[m][:, cols])
+                nc.sync.dma_start(out=sin_sb[m][:, cols], in_=sin_dram[m][:, cols])
+                nc.sync.dma_start(out=cos_sb[m][:, cols], in_=cos_dram[m][:, cols])
         for g in range(KEY_PASSES):
-            v_rows[g] = keep.tile([P, PACK, N], BF16, name="v_rows%d" % g)
-            for u in range(2):
-                nc.sync.dma_start(out=v_rows[g][:, 2 * u : 2 * u + 2, :], in_=v_dram[g][u])
+            load_v(g)
 
         ident = keep.tile([P, P], F32, name="ident")
         make_identity(nc, ident[:])
@@ -94,13 +101,13 @@ def tile_bidirectionalattentionv2_pa_kernel(tc, Q, V, rope_cos, rope_sin, out):
             straight = rope_pool.tile([P, N], F32, name="straight")
             crossed = rope_pool.tile([P, N], F32, name="crossed")
             crossed_halves = crossed[:].rearrange("p (j h a) -> p j h a", j=2, h=2)
-            nc.vector.tensor_tensor(
-                out=straight[:].rearrange("p (j h a) -> p j h a", j=2, h=2), in0=q, in1=cos, op=ALU.mult
-            )
+            nc.gpsimd.tensor_tensor(out=crossed_halves[:, 1], in0=q_in_sbuf[:, 0], in1=sin[:, 1], op=ALU.mult)
             nc.vector.scalar_tensor_tensor(
                 out=crossed_halves[:, 0], in0=q[:, 1], scalar=-1.0, in1=sin[:, 0], op0=ALU.mult, op1=ALU.mult
             )
-            nc.gpsimd.tensor_tensor(out=crossed_halves[:, 1], in0=q_in_sbuf[:, 0], in1=sin[:, 1], op=ALU.mult)
+            nc.vector.tensor_tensor(
+                out=straight[:].rearrange("p (j h a) -> p j h a", j=2, h=2), in0=q, in1=cos, op=ALU.mult
+            )
             summed = other_psum.tile([P, BANK], F32, name="other")
             for j in range(2):
                 for h in range(2):
@@ -128,24 +135,29 @@ def tile_bidirectionalattentionv2_pa_kernel(tc, Q, V, rope_cos, rope_sin, out):
                 in_=summed[:].rearrange("p (t c) -> p c t", t=PACK),
             )
 
-        def quantise_qr(n):
-            c0 = first_column(n)
+        def quantise_qr(first, end):
             nc.vector.quantize_mx(
-                out=qr_codes[:, c0 : c0 + P].bitcast(FP8X4),
-                scales=qr_scales[:, c0 : c0 + P],
-                in_=qr_grouped[:, PACK * c0 : PACK * (c0 + P)],
+                out=qr_codes[:, first:end].bitcast(FP8X4),
+                scales=qr_scales[:, first:end],
+                in_=qr_grouped[:, PACK * first : PACK * end],
             )
 
         v_codes = keep.tile([P, KEY_PASSES * N], U32, name="v_codes", align_bytes=64)
         v_scales = keep.tile([P, KEY_PASSES * N], U8, name="v_scales", align_bytes=64)
         v_grouped = {}
-
-        def regroup_v(g, copy):
+        for g in range(KEY_PASSES):
             v_grouped[g] = keep.tile([P, N * PACK], BF16, name="v_grouped%d" % g, align_bytes=64)
-            copy(
-                out=v_grouped[g][:].rearrange("p (c i t) -> p c t i", i=4, t=PACK),
-                in_=v_rows[g][:].rearrange("p t (c i) -> p c t i", i=4),
-            )
+
+        def regroup_v(g, piece, on_scalar):
+            first = P * piece
+            grouped = v_grouped[g][:, PACK * first : PACK * (first + P)].rearrange("p (c i t) -> p c t i", i=4, t=PACK)
+            rows = v_rows[g][:, :, first : first + P].rearrange("p t (c i) -> p c t i", i=4)
+            if on_scalar:
+                nc.scalar.copy(out=grouped, in_=rows)
+            else:
+                nc.gpsimd.tensor_scalar(
+                    out=grouped, in0=rows, scalar1=1.0, scalar2=0.0, op0=ALU.mult, op1=ALU.add
+                )
 
         def quantise_v(g):
             nc.vector.quantize_mx(
@@ -172,7 +184,7 @@ def tile_bidirectionalattentionv2_pa_kernel(tc, Q, V, rope_cos, rope_sin, out):
 
         def scale_and_min(k, half):
             if half == 0:
-                shifted[k] = soft.tile([P, T], F32, name="shifted")
+                shifted[k] = stat.tile([P, T], F32, name="shifted")
                 lowest[k] = stat.tile([P, HALVES], F32, name="lowest")
             nc.vector.tensor_scalar(
                 out=shifted[k][:, BANK * half : BANK * (half + 1)],
@@ -209,7 +221,11 @@ def tile_bidirectionalattentionv2_pa_kernel(tc, Q, V, rope_cos, rope_sin, out):
                 in_=e_flipped[k][:].rearrange("p (g u q) -> p g q u", g=KEY_PASSES, u=2),
             )
 
+        inverse = {}
+
         def quantise_e(k):
+            inverse[k] = stat.tile([P, 1], F32, name="inverse")
+            nc.vector.reciprocal(out=inverse[k][:], in_=e_sum[k][:])
             e_codes[k] = soft.tile([P, KEY_PASSES * P], U32, name="e_codes", align_bytes=64)
             e_scales[k] = soft.tile([P, KEY_PASSES * P], U8, name="e_scales", align_bytes=64)
             nc.vector.quantize_mx(
@@ -230,46 +246,63 @@ def tile_bidirectionalattentionv2_pa_kernel(tc, Q, V, rope_cos, rope_sin, out):
                 )
 
         def normalise_and_store(k):
-            inverse = stat.tile([P, 1], F32, name="inverse")
-            result = soft.tile([P, N], F32, name="result")
-            nc.vector.reciprocal(out=inverse[:], in_=e_sum[k][:])
-            nc.vector.tensor_scalar(out=result[:], in0=attended[k][:], scalar1=inverse[:], scalar2=None, op0=ALU.mult)
+            result = stat.tile([P, N], F32, name="result")
+            if k in (5,6,):
+                nc.scalar.activation(out=result[:], in_=attended[k][:], func=ACT.Copy, scale=inverse[k][:])
+            else:
+                nc.vector.tensor_scalar(out=result[:], in0=attended[k][:], scalar1=inverse[k][:], scalar2=None, op0=ALU.mult)
             m, i = 2 * (k // 4) + k % 2, (k // 2) % 2
             nc.sync.dma_start(out=out_dram[m][i], in_=result[:])
 
         for n in range(COPY_AHEAD):
             copy_q(n)
         for n in range(TILES):
+            rotate(n)
             if n + COPY_AHEAD < TILES:
                 copy_q(n + COPY_AHEAD)
-            rotate(n)
-        for n in range(TILES - 2):
-            quantise_qr(n)
-        score(0, 0)
-        score(1, 0)
-        regroup_v(0, nc.vector.tensor_copy)
-        quantise_qr(TILES - 2)
+            if n == 5:
+                quantise_qr(0, BANK)
+            if n == 6:
+                score(0, 0)
         scale_and_min(0, 0)
-        quantise_qr(TILES - 1)
-        regroup_v(1, nc.scalar.copy)
+        quantise_qr(BANK, BANK + 2 * P)
+        score(1, 0)
+
+        regroup_v(0, 0, True)
+        quantise_qr(BANK + 2 * P, T)
         score(0, 1)
+        scale_and_min(1, 0)
+        score(1, 1)
+        regroup_v(0, 1, True)
+        regroup_v(0, 2, True)
+        regroup_v(0, 3, False)
+        regroup_v(1, 0, False)
+        regroup_v(1, 1, False)
+        regroup_v(1, 2, False)
+        regroup_v(1, 3, False)
+        scale_and_min(0, 1)
+        scale_and_min(1, 1)
+        score(2, 0)
+        scale_and_min(2, 0)
         for s in range(TILES + OUTPUT_LAG):
-            if s + 2 < TILES:
-                score(s + 2, 0)
-            if s + 1 < TILES:
-                score(s + 1, 1)
-                scale_and_min(s + 1, 0)
-            if s % 2 == 0 and s < QUANTISE_LAG:
-                quantise_v(s // 2)
+            if 0 <= s - 1 < TILES:
+                flip_e(s - 1)
+            if s < TILES:
+                exponential(s)
+
             if 0 <= s - QUANTISE_LAG < TILES:
                 quantise_e(s - QUANTISE_LAG)
-                attend(s - QUANTISE_LAG)
-            if s < TILES:
-                scale_and_min(s, 1)
-            if 0 <= s - EXP_LAG < TILES:
-                exponential(s - EXP_LAG)
-                flip_e(s - EXP_LAG)
-            if 0 <= s - PAIR_LAG < TILES:
-                pair_e(s - PAIR_LAG)
+            if s + 2 < TILES:
+                score(s + 2, 1)
+                scale_and_min(s + 2, 1)
+            if s + 3 < TILES:
+                score(s + 3, 0)
+                scale_and_min(s + 3, 0)
+            if 0 <= s - 1 < TILES:
+                pair_e(s - 1)
+            if 0 <= s < KEY_PASSES + 0:
+                quantise_v(s - 0)
+            if 0 <= s - ATTEND_LAG < TILES:
+                attend(s - ATTEND_LAG)
             if 0 <= s - OUTPUT_LAG < TILES:
                 normalise_and_store(s - OUTPUT_LAG)

@@ -23,7 +23,7 @@ HALVES = T // BANK
 KEY_PASSES = T // K_PASS
 FLOPS = 2 * 2 * T * T * N
 
-COPY_AHEAD = 2
+COPY_AHEAD = 3
 ATTEND_LAG = 3
 QUANTISE_LAG = 3
 OUTPUT_LAG = 4
@@ -148,16 +148,11 @@ def tile_bidirectionalattentionv2_pa_kernel(tc, Q, V, rope_cos, rope_sin, out):
         for g in range(KEY_PASSES):
             v_grouped[g] = keep.tile([P, N * PACK], BF16, name="v_grouped%d" % g, align_bytes=64)
 
-        def regroup_v(g, piece, on_scalar):
+        def regroup_v(g, piece, copy):
             first = P * piece
             grouped = v_grouped[g][:, PACK * first : PACK * (first + P)].rearrange("p (c i t) -> p c t i", i=4, t=PACK)
             rows = v_rows[g][:, :, first : first + P].rearrange("p t (c i) -> p c t i", i=4)
-            if on_scalar:
-                nc.scalar.copy(out=grouped, in_=rows)
-            else:
-                nc.gpsimd.tensor_scalar(
-                    out=grouped, in0=rows, scalar1=1.0, scalar2=0.0, op0=ALU.mult, op1=ALU.add
-                )
+            copy(out=grouped, in_=rows)
 
         def quantise_v(g):
             nc.vector.quantize_mx(
@@ -254,42 +249,43 @@ def tile_bidirectionalattentionv2_pa_kernel(tc, Q, V, rope_cos, rope_sin, out):
             m, i = 2 * (k // 4) + k % 2, (k // 2) % 2
             nc.sync.dma_start(out=out_dram[m][i], in_=result[:])
 
+        warm = other_psum.tile([P, P], F32, name="other")
+        for n in range(2):
+            nc.tensor.matmul(out=warm[:], lhsT=ident[:], rhs=ident[:], start=True, stop=True)
         for n in range(COPY_AHEAD):
             copy_q(n)
         for n in range(TILES):
             rotate(n)
             if n + COPY_AHEAD < TILES:
                 copy_q(n + COPY_AHEAD)
-            if n == 5:
+            if n == 6:
                 quantise_qr(0, BANK)
             if n == 6:
                 score(0, 0)
+        regroup_v(0, 0, nc.vector.tensor_copy)
+        regroup_v(0, 1, nc.vector.tensor_copy)
         scale_and_min(0, 0)
         quantise_qr(BANK, BANK + 2 * P)
         score(1, 0)
-
-        regroup_v(0, 0, True)
         quantise_qr(BANK + 2 * P, T)
         score(0, 1)
         scale_and_min(1, 0)
         score(1, 1)
-        regroup_v(0, 1, True)
-        regroup_v(0, 2, True)
-        regroup_v(0, 3, False)
-        regroup_v(1, 0, False)
-        regroup_v(1, 1, False)
-        regroup_v(1, 2, False)
-        regroup_v(1, 3, False)
+        regroup_v(0, 2, nc.scalar.copy)
+        regroup_v(0, 3, nc.scalar.copy)
+        regroup_v(1, 0, nc.scalar.copy)
+        regroup_v(1, 1, nc.scalar.copy)
         scale_and_min(0, 1)
         scale_and_min(1, 1)
         score(2, 0)
         scale_and_min(2, 0)
+        regroup_v(1, 2, nc.vector.tensor_copy)
+        regroup_v(1, 3, nc.vector.tensor_copy)
         for s in range(TILES + OUTPUT_LAG):
             if 0 <= s - 1 < TILES:
                 flip_e(s - 1)
             if s < TILES:
                 exponential(s)
-
             if 0 <= s - QUANTISE_LAG < TILES:
                 quantise_e(s - QUANTISE_LAG)
             if s + 2 < TILES:

@@ -29,6 +29,8 @@ QUANTISE_LAG = 3
 OUTPUT_LAG = 4
 EARLY = 4
 
+SCALAR_OUT = ()
+
 
 def first_column(n):
     m, i = n // 2, n % 2
@@ -145,8 +147,11 @@ def tile_bidirectionalattentionv2_pa_kernel(tc, Q, V, rope_cos, rope_sin, out):
         v_codes = keep.tile([P, KEY_PASSES * N], U32, name="v_codes", align_bytes=64)
         v_scales = keep.tile([P, KEY_PASSES * N], U8, name="v_scales", align_bytes=64)
         v_grouped = {}
-        for g in range(KEY_PASSES):
-            v_grouped[g] = keep.tile([P, N * PACK], BF16, name="v_grouped%d" % g, align_bytes=64)
+        v_grouped[0] = keep.tile([P, N * PACK], BF16, name="v_grouped0", align_bytes=64)
+        v_grouped[1] = qr_grouped[:, PACK * BANK :]
+
+        def gpsimd_copy(out, in_):
+            nc.gpsimd.tensor_scalar(out=out, in0=in_, scalar1=1.0, scalar2=0.0, op0=ALU.mult, op1=ALU.add)
 
         def regroup_v(g, piece, copy):
             first = P * piece
@@ -158,9 +163,12 @@ def tile_bidirectionalattentionv2_pa_kernel(tc, Q, V, rope_cos, rope_sin, out):
             nc.vector.quantize_mx(
                 out=v_codes[:, N * g : N * (g + 1)].bitcast(FP8X4),
                 scales=v_scales[:, N * g : N * (g + 1)],
-                in_=v_grouped[g][:],
+                in_=v_grouped[g][:, :],
             )
 
+        inverse = {}
+        minus_one = keep.tile([P, 1], F32, name="minus_one")
+        nc.gpsimd.memset(minus_one[:], -1.0)
         banks, shifted, lowest, e_sb, e_sum, e_flipped, e_pairs, e_codes, e_scales, attended = (
             {}, {}, {}, {}, {}, {}, {}, {}, {}, {},
         )
@@ -191,63 +199,86 @@ def tile_bidirectionalattentionv2_pa_kernel(tc, Q, V, rope_cos, rope_sin, out):
                 accum_out=lowest[k][:, half : half + 1],
             )
 
-        def exponential(k):
-            e_sb[k] = soft.tile([P, T], BF16, name="e_sb")
-            e_sum[k] = stat.tile([P, 1], F32, name="e_sum")
+        def exponential(k, half=None):
+            cols = slice(0, T) if half is None else slice(BANK * half, BANK * (half + 1))
+            if not half:
+                e_sb[k] = soft.tile([P, T], BF16, name="e_sb")
+                e_sum[k] = stat.tile([P, HALVES], F32, name="e_sum")
             nc.scalar.activation(
-                out=e_sb[k][:],
-                in_=shifted[k][:],
+                out=e_sb[k][:, cols],
+                in_=shifted[k][:, cols],
                 func=ACT.Exp,
                 bias=lowest[k][:, HALVES - 1 : HALVES],
                 scale=-1.0,
-                accum_out=e_sum[k][:],
+                accum_out=e_sum[k][:, half or 0 : (half or 0) + 1],
             )
-
-        def flip_e(k):
-            words = e_sb[k][:].bitcast(F32)
-            e_flipped[k] = other_psum.tile([P, BANK], F32, name="other")
-            for b in range(PACK):
-                nc.tensor.transpose(e_flipped[k][:, P * b : P * (b + 1)], words[:, P * b : P * (b + 1)], ident[:])
-
-        def pair_e(k):
-            e_pairs[k] = soft.tile([P, BANK], F32, name="e_pairs", align_bytes=64)
-            nc.scalar.copy(
-                out=e_pairs[k][:].rearrange("p (g q u) -> p g q u", g=KEY_PASSES, u=2),
-                in_=e_flipped[k][:].rearrange("p (g u q) -> p g q u", g=KEY_PASSES, u=2),
-            )
-
-        inverse = {}
-
-        def quantise_e(k):
+            if half == 0:
+                return
             inverse[k] = stat.tile([P, 1], F32, name="inverse")
-            nc.vector.reciprocal(out=inverse[k][:], in_=e_sum[k][:])
-            e_codes[k] = soft.tile([P, KEY_PASSES * P], U32, name="e_codes", align_bytes=64)
-            e_scales[k] = soft.tile([P, KEY_PASSES * P], U8, name="e_scales", align_bytes=64)
-            nc.vector.quantize_mx(
-                out=e_codes[k][:].bitcast(FP8X4), scales=e_scales[k][:], in_=e_pairs[k][:].bitcast(BF16)
-            )
+            total = e_sum[k][:, 0:1]
+            if half is not None:
+                both = stat.tile([P, 1], F32, name="both")
+                nc.gpsimd.tensor_tensor(out=both[:], in0=e_sum[k][:, 0:1], in1=e_sum[k][:, 1:2], op=ALU.add)
+                total = both[:]
+            nc.gpsimd.tensor_tensor(out=inverse[k][:], in0=total, in1=minus_one[:], op=ALU.pow)
 
-        def attend(k):
-            attended[k] = other_psum.tile([P, N], F32, name="other")
-            for g in range(KEY_PASSES):
-                nc.tensor.matmul_mx(
-                    out=attended[k][:],
-                    lhsT=e_codes[k][:, P * g : P * (g + 1)].bitcast(FP8X4),
-                    lhsT_scale=e_scales[k][:, P * g : P * (g + 1)],
-                    rhs=v_codes[:, N * g : N * (g + 1)].bitcast(FP8X4),
-                    rhs_scale=v_scales[:, N * g : N * (g + 1)],
-                    start=(g == 0),
-                    stop=(g == KEY_PASSES - 1),
+        def flip_e(k, half=None):
+            words = e_sb[k][:].bitcast(F32)
+            blocks = range(PACK) if half is None else range(2 * half, 2 * half + 2)
+            e_flipped[k, half] = other_psum.tile([P, P * len(blocks)], F32, name="other")
+            for place, b in enumerate(blocks):
+                nc.tensor.transpose(
+                    e_flipped[k, half][:, P * place : P * (place + 1)], words[:, P * b : P * (b + 1)], ident[:]
                 )
 
-        def normalise_and_store(k):
-            result = stat.tile([P, N], F32, name="result")
-            if k in (5,6,):
-                nc.scalar.activation(out=result[:], in_=attended[k][:], func=ACT.Copy, scale=inverse[k][:])
+        def pair_e(k, half=None):
+            if not half:
+                e_pairs[k] = soft.tile([P, BANK], F32, name="e_pairs", align_bytes=64)
+            passes = KEY_PASSES if half is None else 1
+            first = 2 * P * (half or 0)
+            nc.scalar.copy(
+                out=e_pairs[k][:, first : first + 2 * P * passes].rearrange("p (g q u) -> p g q u", g=passes, u=2),
+                in_=e_flipped[k, half][:].rearrange("p (g u q) -> p g q u", g=passes, u=2),
+            )
+
+        def quantise_e(k, half=None):
+            if not half:
+                e_codes[k] = soft.tile([P, KEY_PASSES * P], U32, name="e_codes", align_bytes=64)
+                e_scales[k] = soft.tile([P, KEY_PASSES * P], U8, name="e_scales", align_bytes=64)
+            cols = slice(0, KEY_PASSES * P) if half is None else slice(P * half, P * (half + 1))
+            words = slice(0, BANK) if half is None else slice(2 * P * half, 2 * P * (half + 1))
+            nc.vector.quantize_mx(
+                out=e_codes[k][:, cols].bitcast(FP8X4),
+                scales=e_scales[k][:, cols],
+                in_=e_pairs[k][:, words].bitcast(BF16),
+            )
+
+        def attend(k, g, side=None):
+            cols = slice(0, N) if side is None else slice(N // 2 * side, N // 2 * (side + 1))
+            width = N if side is None else N // 2
+            if g == 0:
+                attended[k, side] = other_psum.tile([P, width], F32, name="other")
+            nc.tensor.matmul_mx(
+                out=attended[k, side][:],
+                lhsT=e_codes[k][:, P * g : P * (g + 1)].bitcast(FP8X4),
+                lhsT_scale=e_scales[k][:, P * g : P * (g + 1)],
+                rhs=v_codes[:, N * g + cols.start : N * g + cols.stop].bitcast(FP8X4),
+                rhs_scale=v_scales[:, N * g + cols.start : N * g + cols.stop],
+                start=(g == 0),
+                stop=(g == KEY_PASSES - 1),
+            )
+
+        def normalise_and_store(k, on_scalar, side=None):
+            cols = slice(0, N) if side is None else slice(N // 2 * side, N // 2 * (side + 1))
+            result = stat.tile([P, cols.stop - cols.start], F32, name="result")
+            if on_scalar:
+                nc.scalar.activation(out=result[:], in_=attended[k, side][:], func=ACT.Copy, scale=inverse[k][:])
             else:
-                nc.vector.tensor_scalar(out=result[:], in0=attended[k][:], scalar1=inverse[k][:], scalar2=None, op0=ALU.mult)
+                nc.vector.tensor_scalar(
+                    out=result[:], in0=attended[k, side][:], scalar1=inverse[k][:], scalar2=None, op0=ALU.mult
+                )
             m, i = 2 * (k // 4) + k % 2, (k // 2) % 2
-            nc.sync.dma_start(out=out_dram[m][i], in_=result[:])
+            nc.sync.dma_start(out=out_dram[m][i][:, cols], in_=result[:])
 
         warm = other_psum.tile([P, P], F32, name="other")
         for n in range(2):
@@ -258,47 +289,70 @@ def tile_bidirectionalattentionv2_pa_kernel(tc, Q, V, rope_cos, rope_sin, out):
             rotate(n)
             if n + COPY_AHEAD < TILES:
                 copy_q(n + COPY_AHEAD)
-            if n == 6:
-                quantise_qr(0, BANK)
-            if n == 6:
-                score(0, 0)
-        regroup_v(0, 0, nc.vector.tensor_copy)
-        regroup_v(0, 1, nc.vector.tensor_copy)
-        scale_and_min(0, 0)
-        quantise_qr(BANK, BANK + 2 * P)
+        quantise_qr(0, BANK)
+        score(0, 0)
         score(1, 0)
+        quantise_qr(BANK, BANK + 2 * P)
+        scale_and_min(0, 0)
+        regroup_v(0, 0, nc.scalar.copy)
         quantise_qr(BANK + 2 * P, T)
         score(0, 1)
         scale_and_min(1, 0)
         score(1, 1)
-        regroup_v(0, 2, nc.scalar.copy)
-        regroup_v(0, 3, nc.scalar.copy)
-        regroup_v(1, 0, nc.scalar.copy)
-        regroup_v(1, 1, nc.scalar.copy)
+        for piece in range(1, 3):
+            regroup_v(0, piece, nc.scalar.copy)
         scale_and_min(0, 1)
         scale_and_min(1, 1)
+        for piece in (2, 3, 0, 1):
+            regroup_v(1, piece, gpsimd_copy)
         score(2, 0)
         scale_and_min(2, 0)
-        regroup_v(1, 2, nc.vector.tensor_copy)
-        regroup_v(1, 3, nc.vector.tensor_copy)
-        for s in range(TILES + OUTPUT_LAG):
-            if 0 <= s - 1 < TILES:
+        for s in range(TILES):
+            if s > 0:
                 flip_e(s - 1)
-            if s < TILES:
+            if s < TILES - 1:
                 exponential(s)
-            if 0 <= s - QUANTISE_LAG < TILES:
+            else:
+                exponential(s, 0)
+                exponential(s, 1)
+            if s == 0:
+                regroup_v(0, 3, nc.scalar.copy)
+            if 0 <= s - QUANTISE_LAG:
                 quantise_e(s - QUANTISE_LAG)
             if s + 2 < TILES:
                 score(s + 2, 1)
-                scale_and_min(s + 2, 1)
             if s + 3 < TILES:
                 score(s + 3, 0)
                 scale_and_min(s + 3, 0)
-            if 0 <= s - 1 < TILES:
+            if s + 2 < TILES:
+                scale_and_min(s + 2, 1)
+            if s > 0:
                 pair_e(s - 1)
-            if 0 <= s < KEY_PASSES + 0:
-                quantise_v(s - 0)
-            if 0 <= s - ATTEND_LAG < TILES:
-                attend(s - ATTEND_LAG)
-            if 0 <= s - OUTPUT_LAG < TILES:
-                normalise_and_store(s - OUTPUT_LAG)
+            if 1 <= s < KEY_PASSES + 1:
+                quantise_v(s - 1)
+            if 0 <= s - ATTEND_LAG:
+                for g in range(KEY_PASSES):
+                    attend(s - ATTEND_LAG, g)
+            if 0 <= s - OUTPUT_LAG and s - OUTPUT_LAG not in SCALAR_OUT:
+                normalise_and_store(s - OUTPUT_LAG, False)
+            if s - 5 in SCALAR_OUT:
+                normalise_and_store(s - 5, True)
+        last = TILES - 1
+        for half in range(HALVES):
+            flip_e(last, half)
+            pair_e(last, half)
+        quantise_e(last - 2)
+        attend(last - 2, 0)
+        attend(last - 2, 1)
+        normalise_and_store(last - 3, False)
+        quantise_e(last - 1)
+        attend(last - 1, 0)
+        attend(last - 1, 1)
+        for g in range(KEY_PASSES):
+            quantise_e(last, g)
+            for side in range(2):
+                attend(last, g, side)
+        normalise_and_store(last - 2, False)
+        normalise_and_store(last - 1, True)
+        normalise_and_store(last, False, 0)
+        normalise_and_store(last, True, 1)

@@ -25,8 +25,8 @@ FLOPS = 2 * 2 * T * T * N
 
 COPY_AHEAD = 3
 ATTEND_LAG = 3
-QUANTISE_LAG = 3
-OUTPUT_LAG = 4
+QUANTISE_LAG = 2
+OUTPUT_LAG = 3
 EARLY = 4
 
 SCALAR_OUT = ()
@@ -62,7 +62,7 @@ def tile_bidirectionalattentionv2_pa_kernel(tc, Q, V, rope_cos, rope_sin, out):
             q_sb[m] = keep.tile([P, 2 * N], BF16, name="q%d" % m)
             cos_sb[m] = keep.tile([P, 2 * N], BF16, name="cos%d" % m)
             sin_sb[m] = keep.tile([P, 2 * N], BF16, name="sin%d" % m)
-            width = N if m < 4 else 2 * N
+            width = N if m == CHUNKS - 1 else 2 * N
             for first in range(0, 2 * N, width):
                 cols = slice(first, first + width)
                 nc.sync.dma_start(out=q_sb[m][:, cols], in_=q_dram[m][:, cols])
@@ -341,18 +341,16 @@ def tile_bidirectionalattentionv2_pa_kernel(tc, Q, V, rope_cos, rope_sin, out):
         for half in range(HALVES):
             flip_e(last, half)
             pair_e(last, half)
-        quantise_e(last - 2)
-        attend(last - 2, 0)
-        attend(last - 2, 1)
-        normalise_and_store(last - 3, False)
-        quantise_e(last - 1)
-        attend(last - 1, 0)
-        attend(last - 1, 1)
+        attend(5, 0)
+        attend(5, 1)
+        quantise_e(6)
+        attend(6, 0)
+        attend(6, 1)
         for g in range(KEY_PASSES):
             quantise_e(last, g)
             for side in range(2):
                 attend(last, g, side)
-        normalise_and_store(last - 2, False)
-        normalise_and_store(last - 1, True)
+        normalise_and_store(5, False)
+        normalise_and_store(6, True)
         normalise_and_store(last, False, 0)
         normalise_and_store(last, True, 1)

@@ -62,12 +62,11 @@ def tile_bidirectionalattentionv2_pa_kernel(tc, Q, V, rope_cos, rope_sin, out):
             q_sb[m] = keep.tile([P, 2 * N], BF16, name="q%d" % m)
             cos_sb[m] = keep.tile([P, 2 * N], BF16, name="cos%d" % m)
             sin_sb[m] = keep.tile([P, 2 * N], BF16, name="sin%d" % m)
+            nc.sync.dma_start(out=q_sb[m][:], in_=q_dram[m])
+            nc.sync.dma_start(out=sin_sb[m][:], in_=sin_dram[m])
             width = N if m == CHUNKS - 1 else 2 * N
             for first in range(0, 2 * N, width):
-                cols = slice(first, first + width)
-                nc.sync.dma_start(out=q_sb[m][:, cols], in_=q_dram[m][:, cols])
-                nc.sync.dma_start(out=sin_sb[m][:, cols], in_=sin_dram[m][:, cols])
-                nc.sync.dma_start(out=cos_sb[m][:, cols], in_=cos_dram[m][:, cols])
+                nc.sync.dma_start(out=cos_sb[m][:, first : first + width], in_=cos_dram[m][:, first : first + width])
         for g in range(KEY_PASSES):
             load_v(g)
 
@@ -328,8 +327,8 @@ def tile_bidirectionalattentionv2_pa_kernel(tc, Q, V, rope_cos, rope_sin, out):
                 scale_and_min(s + 2, 1)
             if s > 0:
                 pair_e(s - 1)
-            if 1 <= s < KEY_PASSES + 1:
-                quantise_v(s - 1)
+            if 0 <= s < KEY_PASSES + 0:
+                quantise_v(s - 0)
             if 0 <= s - ATTEND_LAG:
                 for g in range(KEY_PASSES):
                     attend(s - ATTEND_LAG, g)

@@ -29,7 +29,8 @@ QUANTISE_LAG = 2
 OUTPUT_LAG = 3
 EARLY = 4
 
-SCALAR_OUT = ()
+SCALAR_OUT = (1,)
+LATE = 5
 
 
 def first_column(n):
@@ -106,9 +107,14 @@ def tile_bidirectionalattentionv2_pa_kernel(tc, Q, V, rope_cos, rope_sin, out):
             nc.vector.scalar_tensor_tensor(
                 out=crossed_halves[:, 0], in0=q[:, 1], scalar=-1.0, in1=sin[:, 0], op0=ALU.mult, op1=ALU.mult
             )
-            nc.vector.tensor_tensor(
-                out=straight[:].rearrange("p (j h a) -> p j h a", j=2, h=2), in0=q, in1=cos, op=ALU.mult
-            )
+            parts = (slice(0, 1), slice(1, 2)) if n == TILES - 1 else (slice(0, 2),)
+            for part in parts:
+                nc.vector.tensor_tensor(
+                    out=straight[:].rearrange("p (j h a) -> p j h a", j=2, h=2)[:, part],
+                    in0=q[:, part],
+                    in1=cos[:, part],
+                    op=ALU.mult,
+                )
             summed = other_psum.tile([P, BANK], F32, name="other")
             for j in range(2):
                 for h in range(2):
@@ -256,7 +262,10 @@ def tile_bidirectionalattentionv2_pa_kernel(tc, Q, V, rope_cos, rope_sin, out):
             cols = slice(0, N) if side is None else slice(N // 2 * side, N // 2 * (side + 1))
             width = N if side is None else N // 2
             if g == 0:
-                attended[k, side] = other_psum.tile([P, width], F32, name="other")
+                if k < LATE:
+                    attended[k, side] = other_psum.tile([P, width], F32, name="other")
+                else:
+                    attended[k, side] = score_psum.tile([P, width], F32, name="bank")
             nc.tensor.matmul_mx(
                 out=attended[k, side][:],
                 lhsT=e_codes[k][:, P * g : P * (g + 1)].bitcast(FP8X4),
@@ -301,11 +310,13 @@ def tile_bidirectionalattentionv2_pa_kernel(tc, Q, V, rope_cos, rope_sin, out):
         for piece in range(1, 3):
             regroup_v(0, piece, nc.scalar.copy)
         scale_and_min(0, 1)
-        scale_and_min(1, 1)
-        for piece in (2, 3, 0, 1):
-            regroup_v(1, piece, gpsimd_copy)
         score(2, 0)
         scale_and_min(2, 0)
+        scale_and_min(1, 1)
+        regroup_v(1, 2, gpsimd_copy)
+        regroup_v(0, 3, gpsimd_copy)
+        for piece in (3, 0, 1):
+            regroup_v(1, piece, gpsimd_copy)
         for s in range(TILES):
             if s > 0:
                 flip_e(s - 1)
@@ -314,17 +325,14 @@ def tile_bidirectionalattentionv2_pa_kernel(tc, Q, V, rope_cos, rope_sin, out):
             else:
                 exponential(s, 0)
                 exponential(s, 1)
-            if s == 0:
-                regroup_v(0, 3, nc.scalar.copy)
             if 0 <= s - QUANTISE_LAG:
                 quantise_e(s - QUANTISE_LAG)
             if s + 2 < TILES:
                 score(s + 2, 1)
+                scale_and_min(s + 2, 1)
             if s + 3 < TILES:
                 score(s + 3, 0)
                 scale_and_min(s + 3, 0)
-            if s + 2 < TILES:
-                scale_and_min(s + 2, 1)
             if s > 0:
                 pair_e(s - 1)
             if 0 <= s < KEY_PASSES + 0:
@@ -334,22 +342,22 @@ def tile_bidirectionalattentionv2_pa_kernel(tc, Q, V, rope_cos, rope_sin, out):
                     attend(s - ATTEND_LAG, g)
             if 0 <= s - OUTPUT_LAG and s - OUTPUT_LAG not in SCALAR_OUT:
                 normalise_and_store(s - OUTPUT_LAG, False)
-            if s - 5 in SCALAR_OUT:
-                normalise_and_store(s - 5, True)
+            if s - 4 in SCALAR_OUT:
+                normalise_and_store(s - 4, True)
         last = TILES - 1
+        attend(5, 0)
+        attend(5, 1)
         for half in range(HALVES):
             flip_e(last, half)
             pair_e(last, half)
-        attend(5, 0)
-        attend(5, 1)
         quantise_e(6)
         attend(6, 0)
         attend(6, 1)
+        normalise_and_store(5, False)
         for g in range(KEY_PASSES):
             quantise_e(last, g)
             for side in range(2):
                 attend(last, g, side)
-        normalise_and_store(5, False)
-        normalise_and_store(6, True)
+        normalise_and_store(6, False)
         normalise_and_store(last, False, 0)
         normalise_and_store(last, True, 1)

import math

import concourse.mybir as mybir
from concourse.masks import make_identity

F32 = mybir.dt.float32
BF16 = mybir.dt.bfloat16
U32 = mybir.dt.uint32
U8 = mybir.dt.uint8
FP8X4 = mybir.dt.float8_e4m3fn_x4
ALU = mybir.AluOpType
ACT = mybir.ActivationFunctionType

P = 128
T = 1024
N = 512
PACK = 4
K_PASS = P * PACK
BANK = 512
CHUNKS = T // (2 * P)
TILES = T // P
HALVES = T // BANK
KEY_PASSES = T // K_PASS
FLOPS = 2 * 2 * T * T * N

COPY_AHEAD = 3
ATTEND_LAG = 3
QUANTISE_LAG = 2
OUTPUT_LAG = 3
EARLY = 4

SCALAR_OUT = (1,)
LATE = 5


def first_column(n):
    m, i = n // 2, n % 2
    return K_PASS * (m // 2) + 2 * P * i + P * (m % 2)


def tile_bidirectionalattentionv2_pa_kernel(tc, Q, V, rope_cos, rope_sin, out):
    nc = tc.nc
    by_chunk = "(m p i) f -> m p (i f)"
    q_dram = Q.flatten_outer_dims().rearrange(by_chunk, m=CHUNKS, i=2)
    cos_dram = rope_cos.flatten_outer_dims().rearrange(by_chunk, m=CHUNKS, i=2)
    sin_dram = rope_sin.flatten_outer_dims().rearrange(by_chunk, m=CHUNKS, i=2)
    v_dram = V.flatten_outer_dims().rearrange("(g p e u) f -> g u p e f", g=KEY_PASSES, e=2, u=2)
    out_dram = out.flatten_outer_dims().rearrange("(m p i) f -> m i p f", m=CHUNKS, i=2)

    with tc.tile_pool(name="keep", bufs=1) as keep, tc.tile_pool(name="rope", bufs=4) as rope_pool, tc.tile_pool(
        name="soft", bufs=4
    ) as soft, tc.tile_pool(name="stat", bufs=TILES) as stat, tc.psum_pool(name="score", bufs=4) as score_psum, tc.psum_pool(
        name="other", bufs=4
    ) as other_psum, tc.manual_schedule():
        q_sb, cos_sb, sin_sb, v_rows = {}, {}, {}, {}

        def load_v(g):
            v_rows[g] = keep.tile([P, PACK, N], BF16, name="v_rows%d" % g)
            for u in range(2):
                nc.sync.dma_start(out=v_rows[g][:, 2 * u : 2 * u + 2, :], in_=v_dram[g][u])

        for m in range(CHUNKS):
            q_sb[m] = keep.tile([P, 2 * N], BF16, name="q%d" % m)
            cos_sb[m] = keep.tile([P, 2 * N], BF16, name="cos%d" % m)
            sin_sb[m] = keep.tile([P, 2 * N], BF16, name="sin%d" % m)
            nc.sync.dma_start(out=q_sb[m][:], in_=q_dram[m])
            nc.sync.dma_start(out=sin_sb[m][:], in_=sin_dram[m])
            width = N if m == CHUNKS - 1 else 2 * N
            for first in range(0, 2 * N, width):
                nc.sync.dma_start(out=cos_sb[m][:, first : first + width], in_=cos_dram[m][:, first : first + width])
        for g in range(KEY_PASSES):
            load_v(g)

        ident = keep.tile([P, P], F32, name="ident")
        make_identity(nc, ident[:])
        ident_bf = keep.tile([P, P], BF16, name="ident_bf")
        make_identity(nc, ident_bf[:])
        zero = keep.tile([P, 1], F32, name="zero")
        one = keep.tile([P, 1], F32, name="one")
        nc.vector.memset(zero[:], 0.0)
        nc.scalar.activation(out=one[:], in_=zero[:], func=ACT.Exp)

        qr_grouped = keep.tile([P, T * PACK], BF16, name="qr_grouped", align_bytes=64)
        qr_codes = keep.tile([P, T], U32, name="qr_codes", align_bytes=64)
        qr_scales = keep.tile([P, T], U8, name="qr_scales", align_bytes=64)

        q_psum = {}

        def copy_q(n):
            m, i = n // 2, n % 2
            q_psum[n] = score_psum.tile([P, BANK], F32, name="bank")
            nc.tensor.matmul(
                out=q_psum[n][:], lhsT=ident_bf[:], rhs=q_sb[m][:, N * i : N * (i + 1)], start=True, stop=True
            )

        def rotate(n):
            m, i = n // 2, n % 2
            split = "p (a h j) -> p j h a"
            q = q_psum[n][:].rearrange(split, h=2, j=2)
            q_in_sbuf = q_sb[m][:, N * i : N * (i + 1)].rearrange(split, h=2, j=2)
            cos = cos_sb[m][:, N * i : N * (i + 1)].rearrange(split, h=2, j=2)
            sin = sin_sb[m][:, N * i : N * (i + 1)].rearrange(split, h=2, j=2)
            straight = rope_pool.tile([P, N], F32, name="straight")
            crossed = rope_pool.tile([P, N], F32, name="crossed")
            crossed_halves = crossed[:].rearrange("p (j h a) -> p j h a", j=2, h=2)
            nc.gpsimd.tensor_tensor(out=crossed_halves[:, 1], in0=q_in_sbuf[:, 0], in1=sin[:, 1], op=ALU.mult)
            nc.vector.scalar_tensor_tensor(
                out=crossed_halves[:, 0], in0=q[:, 1], scalar=-1.0, in1=sin[:, 0], op0=ALU.mult, op1=ALU.mult
            )
            parts = (slice(0, 1), slice(1, 2)) if n == TILES - 1 else (slice(0, 2),)
            for part in parts:
                nc.vector.tensor_tensor(
                    out=straight[:].rearrange("p (j h a) -> p j h a", j=2, h=2)[:, part],
                    in0=q[:, part],
                    in1=cos[:, part],
                    op=ALU.mult,
                )
            summed = other_psum.tile([P, BANK], F32, name="other")
            for j in range(2):
                for h in range(2):
                    t = 2 * h + j
                    first = P * (2 * j + h)
                    nc.tensor.matmul(
                        out=summed[:, P * t : P * (t + 1)],
                        lhsT=straight[:, first : first + P],
                        rhs=ident[:],
                        start=True,
                        stop=False,
                        is_transpose=True,
                    )
                    nc.tensor.matmul(
                        out=summed[:, P * t : P * (t + 1)],
                        lhsT=crossed[:, first : first + P],
                        rhs=ident[:],
                        start=False,
                        stop=True,
                        is_transpose=True,
                    )
            c0 = first_column(n)
            nc.scalar.copy(
                out=qr_grouped[:, PACK * c0 : PACK * (c0 + P)].rearrange("p (c t) -> p c t", t=PACK),
                in_=summed[:].rearrange("p (t c) -> p c t", t=PACK),
            )

        def quantise_qr(first, end):
            nc.vector.quantize_mx(
                out=qr_codes[:, first:end].bitcast(FP8X4),
                scales=qr_scales[:, first:end],
                in_=qr_grouped[:, PACK * first : PACK * end],
            )

        v_codes = keep.tile([P, KEY_PASSES * N], U32, name="v_codes", align_bytes=64)
        v_scales = keep.tile([P, KEY_PASSES * N], U8, name="v_scales", align_bytes=64)
        v_grouped = {}
        v_grouped[0] = keep.tile([P, N * PACK], BF16, name="v_grouped0", align_bytes=64)
        v_grouped[1] = qr_grouped[:, PACK * BANK :]

        def gpsimd_copy(out, in_):
            nc.gpsimd.tensor_scalar(out=out, in0=in_, scalar1=1.0, scalar2=0.0, op0=ALU.mult, op1=ALU.add)

        def regroup_v(g, piece, copy):
            first = P * piece
            grouped = v_grouped[g][:, PACK * first : PACK * (first + P)].rearrange("p (c i t) -> p c t i", i=4, t=PACK)
            rows = v_rows[g][:, :, first : first + P].rearrange("p t (c i) -> p c t i", i=4)
            copy(out=grouped, in_=rows)

        def quantise_v(g):
            nc.vector.quantize_mx(
                out=v_codes[:, N * g : N * (g + 1)].bitcast(FP8X4),
                scales=v_scales[:, N * g : N * (g + 1)],
                in_=v_grouped[g][:, :],
            )

        inverse = {}
        minus_one = keep.tile([P, 1], F32, name="minus_one")
        nc.gpsimd.memset(minus_one[:], -1.0)
        banks, shifted, lowest, e_sb, e_sum, e_flipped, e_pairs, e_codes, e_scales, attended = (
            {}, {}, {}, {}, {}, {}, {}, {}, {}, {},
        )

        def score(k, half):
            banks[k, half] = score_psum.tile([P, BANK], F32, name="bank")
            nc.tensor.matmul_mx(
                out=banks[k, half][:],
                lhsT=qr_codes[:, P * k : P * (k + 1)].bitcast(FP8X4),
                lhsT_scale=qr_scales[:, P * k : P * (k + 1)],
                rhs=qr_codes[:, BANK * half : BANK * (half + 1)].bitcast(FP8X4),
                rhs_scale=qr_scales[:, BANK * half : BANK * (half + 1)],
                start=True,
                stop=True,
            )

        def scale_and_min(k, half):
            if half == 0:
                shifted[k] = stat.tile([P, T], F32, name="shifted")
                lowest[k] = stat.tile([P, HALVES], F32, name="lowest")
            nc.vector.tensor_scalar(
                out=shifted[k][:, BANK * half : BANK * (half + 1)],
                in0=banks[k, half][:],
                scalar1=-1.0 / math.sqrt(N),
                scalar2=None if half == 0 else lowest[k][:, half - 1 : half],
                op0=ALU.mult,
                op1=ALU.min,
                accum_out=lowest[k][:, half : half + 1],
            )

        def exponential(k, half=None):
            cols = slice(0, T) if half is None else slice(BANK * half, BANK * (half + 1))
            if not half:
                e_sb[k] = soft.tile([P, T], BF16, name="e_sb")
                e_sum[k] = stat.tile([P, HALVES], F32, name="e_sum")
            nc.scalar.activation(
                out=e_sb[k][:, cols],
                in_=shifted[k][:, cols],
                func=ACT.Exp,
                bias=lowest[k][:, HALVES - 1 : HALVES],
                scale=-1.0,
                accum_out=e_sum[k][:, half or 0 : (half or 0) + 1],
            )
            if half == 0:
                return
            inverse[k] = stat.tile([P, 1], F32, name="inverse")
            total = e_sum[k][:, 0:1]
            if half is not None:
                both = stat.tile([P, 1], F32, name="both")
                nc.gpsimd.tensor_tensor(out=both[:], in0=e_sum[k][:, 0:1], in1=e_sum[k][:, 1:2], op=ALU.add)
                total = both[:]
            nc.gpsimd.tensor_tensor(out=inverse[k][:], in0=total, in1=minus_one[:], op=ALU.pow)

        def flip_e(k, half=None):
            words = e_sb[k][:].bitcast(F32)
            blocks = range(PACK) if half is None else range(2 * half, 2 * half + 2)
            e_flipped[k, half] = other_psum.tile([P, P * len(blocks)], F32, name="other")
            for place, b in enumerate(blocks):
                nc.tensor.transpose(
                    e_flipped[k, half][:, P * place : P * (place + 1)], words[:, P * b : P * (b + 1)], ident[:]
                )

        def pair_e(k, half=None):
            if not half:
                e_pairs[k] = soft.tile([P, BANK], F32, name="e_pairs", align_bytes=64)
            passes = KEY_PASSES if half is None else 1
            first = 2 * P * (half or 0)
            nc.scalar.copy(
                out=e_pairs[k][:, first : first + 2 * P * passes].rearrange("p (g q u) -> p g q u", g=passes, u=2),
                in_=e_flipped[k, half][:].rearrange("p (g u q) -> p g q u", g=passes, u=2),
            )

        def quantise_e(k, half=None):
            if not half:
                e_codes[k] = soft.tile([P, KEY_PASSES * P], U32, name="e_codes", align_bytes=64)
                e_scales[k] = soft.tile([P, KEY_PASSES * P], U8, name="e_scales", align_bytes=64)
            cols = slice(0, KEY_PASSES * P) if half is None else slice(P * half, P * (half + 1))
            words = slice(0, BANK) if half is None else slice(2 * P * half, 2 * P * (half + 1))
            nc.vector.quantize_mx(
                out=e_codes[k][:, cols].bitcast(FP8X4),
                scales=e_scales[k][:, cols],
                in_=e_pairs[k][:, words].bitcast(BF16),
            )

        def attend(k, g, side=None):
            cols = slice(0, N) if side is None else slice(N // 2 * side, N // 2 * (side + 1))
            width = N if side is None else N // 2
            if g == 0:
                if k < LATE:
                    attended[k, side] = other_psum.tile([P, width], F32, name="other")
                else:
                    attended[k, side] = score_psum.tile([P, width], F32, name="bank")
            nc.tensor.matmul_mx(
                out=attended[k, side][:],
                lhsT=e_codes[k][:, P * g : P * (g + 1)].bitcast(FP8X4),
                lhsT_scale=e_scales[k][:, P * g : P * (g + 1)],
                rhs=v_codes[:, N * g + cols.start : N * g + cols.stop].bitcast(FP8X4),
                rhs_scale=v_scales[:, N * g + cols.start : N * g + cols.stop],
                start=(g == 0),
                stop=(g == KEY_PASSES - 1),
            )

        def normalise_and_store(k, on_scalar, side=None):
            cols = slice(0, N) if side is None else slice(N // 2 * side, N // 2 * (side + 1))
            result = stat.tile([P, cols.stop - cols.start], F32, name="result")
            if on_scalar:
                nc.scalar.activation(out=result[:], in_=attended[k, side][:], func=ACT.Copy, scale=inverse[k][:])
            else:
                nc.vector.tensor_scalar(
                    out=result[:], in0=attended[k, side][:], scalar1=inverse[k][:], scalar2=None, op0=ALU.mult
                )
            m, i = 2 * (k // 4) + k % 2, (k // 2) % 2
            nc.sync.dma_start(out=out_dram[m][i][:, cols], in_=result[:])

        warm = other_psum.tile([P, P], F32, name="other")
        for n in range(2):
            nc.tensor.matmul(out=warm[:], lhsT=ident[:], rhs=ident[:], start=True, stop=True)
        for n in range(COPY_AHEAD):
            copy_q(n)
        for n in range(TILES):
            rotate(n)
            if n + COPY_AHEAD < TILES:
                copy_q(n + COPY_AHEAD)
        quantise_qr(0, BANK)
        score(0, 0)
        score(1, 0)
        quantise_qr(BANK, BANK + 2 * P)
        scale_and_min(0, 0)
        regroup_v(0, 0, nc.scalar.copy)
        quantise_qr(BANK + 2 * P, T)
        score(0, 1)
        scale_and_min(1, 0)
        score(1, 1)
        for piece in range(1, 3):
            regroup_v(0, piece, nc.scalar.copy)
        scale_and_min(0, 1)
        score(2, 0)
        scale_and_min(2, 0)
        scale_and_min(1, 1)
        regroup_v(1, 2, gpsimd_copy)
        regroup_v(0, 3, gpsimd_copy)
        for piece in (3, 0, 1):
            regroup_v(1, piece, gpsimd_copy)
        for s in range(TILES):
            if s > 0:
                flip_e(s - 1)
            if s < TILES - 1:
                exponential(s)
            else:
                exponential(s, 0)
                exponential(s, 1)
            if 0 <= s - QUANTISE_LAG:
                quantise_e(s - QUANTISE_LAG)
            if s + 2 < TILES:
                score(s + 2, 1)
                scale_and_min(s + 2, 1)
            if s + 3 < TILES:
                score(s + 3, 0)
                scale_and_min(s + 3, 0)
            if s > 0:
                pair_e(s - 1)
            if 0 <= s < KEY_PASSES + 0:
                quantise_v(s - 0)
            if 0 <= s - ATTEND_LAG:
                for g in range(KEY_PASSES):
                    attend(s - ATTEND_LAG, g)
            if 0 <= s - OUTPUT_LAG and s - OUTPUT_LAG not in SCALAR_OUT:
                normalise_and_store(s - OUTPUT_LAG, False)
            if s - 4 in SCALAR_OUT:
                normalise_and_store(s - 4, True)
        last = TILES - 1
        attend(5, 0)
        attend(5, 1)
        for half in range(HALVES):
            flip_e(last, half)
            pair_e(last, half)
        quantise_e(6)
        attend(6, 0)
        attend(6, 1)
        normalise_and_store(5, False)
        for g in range(KEY_PASSES):
            quantise_e(last, g)
            for side in range(2):
                attend(last, g, side)
        normalise_and_store(6, False)
        normalise_and_store(last, False, 0)
        normalise_and_store(last, True, 1)
